import numpy as np
import ml_dtypes

BF16 = ml_dtypes.bfloat16


def bf(x):
    return np.asarray(x, np.float32).astype(BF16)


def f32(x):
    return np.asarray(x, np.float32)


def f64(x):
    return np.asarray(x).astype(np.float64)


def striped(idx):
    return np.tile(idx.reshape(-1, 16).T, (8, 1))


S, D, N, NH, HD, E, M, K, H = 1024, 128, 2048, 2, 128, 256, 512, 4, 512
GAIN = 1.5
NEG = -1e9


def setup_inputs():
    return {
        "table": bf(np.random.standard_normal((D, S))),
        "w_tok": bf(GAIN * np.random.standard_normal((D, M)) / np.sqrt(E)),
        "pos": bf(np.random.standard_normal((D, N))),
        "w_pos": bf(GAIN * np.random.standard_normal((D, M)) / np.sqrt(E)),
        "bq": f32(0.1 * np.random.standard_normal((E, 1))),
        "bv": f32(0.1 * np.random.standard_normal((HD, 1))),
        "mask": f32(np.triu(np.ones((N, N)))),
        "w_o": bf(GAIN * np.random.standard_normal((E, E)) / np.sqrt(E)),
        "b_o": f32(0.1 * np.random.standard_normal((E, 1))),
        "offs": striped(np.concatenate([np.random.permutation(S)[:H] for _ in range(K)])),
    }


def reference(table, w_tok, pos, w_pos, bq, bv, mask, w_o, b_o, offs):
    idx = offs[:16].T.reshape(-1)
    p = f64(w_tok).T @ f64(table)[:, idx] + f64(w_pos).T @ f64(pos)
    qry = p[:E] + f64(bq)
    key = p[E:E + HD]
    val = p[E + HD:] + f64(bv)
    mk = f64(mask)
    att = np.empty((E, N), np.float64)
    for a in range(NH):
        s = key.T @ qry[a * HD:(a + 1) * HD] / np.sqrt(HD)
        s = np.where(mk == 0.0, NEG, s)
        e = np.exp(s - s.max(axis=0, keepdims=True))
        att[a * HD:(a + 1) * HD] = val @ (e / e.sum(axis=0, keepdims=True))
    return f64(w_o).T @ att + f64(b_o)

@@ -1,0 +1,184 @@
+import concourse.mybir as mybir
+from concourse.masks import make_identity
+
+BF16, F32, U16 = mybir.dt.bfloat16, mybir.dt.float32, mybir.dt.uint16
+ALU = mybir.AluOpType
+FUNC = mybir.ActivationFunctionType
+
+P = 128
+WORDS = 1024
+TOKENS = 2048
+HEADS = 2
+BLOCKS = TOKENS // P
+PIECE = 512
+PIECES = TOKENS // PIECE
+KEY, VAL = HEADS, HEADS + 1
+FLIPS = 8
+VPITCH = 136
+SCALE = P ** -0.5
+MASKED = 1.0e9
+
+PAIRS = TOKENS * (TOKENS + 1) // 2
+FLOPS = 2 * (2 * P) * (4 * P) * TOKENS + HEADS * 2 * (2 * P * PAIRS) + 2 * (2 * P) * (2 * P) * TOKENS
+BYTES = (2 * (P * WORDS + 2 * P * 4 * P + P * TOKENS + 4 * P * P) + 4 * (5 * P) + 2 * P * (TOKENS // 16)
+         + 4 * BLOCKS * P * P + 4 * 2 * P * TOKENS)
+
+
+def tile_mytransformer_b_kernel(tc, table, w_tok, pos, w_pos, bq, bv, mask, w_o, b_o, offs, out):
+    nc = tc.nc
+    with (
+        tc.tile_pool(name="held", bufs=1) as held,
+        tc.tile_pool(name="rows", bufs=3) as rows,
+        tc.tile_pool(name="small", bufs=4) as small,
+        tc.psum_pool(name="wide", bufs=4) as wide,
+        tc.psum_pool(name="flip", bufs=2) as flip,
+        tc.psum_pool(name="sums", bufs=2) as sums,
+    ):
+        table_sb = held.tile([P, WORDS], BF16, name="table_sb")
+        offsets = held.tile([P, TOKENS // 16], U16, name="offsets")
+        w_tok_sb = held.tile([P, 4 * P], BF16, name="w_tok_sb")
+        w_pos_sb = held.tile([P, 4 * P], BF16, name="w_pos_sb")
+        pos_sb = held.tile([P, TOKENS], BF16, name="pos_sb")
+        w_o_sb = held.tile([P, HEADS, 2 * P], BF16, name="w_o_sb")
+        bq_sb = held.tile([P, HEADS], F32, name="bq_sb")
+        bv_sb = held.tile([P, 1], F32, name="bv_sb")
+        bo_sb = held.tile([P, 2], F32, name="bo_sb")
+        mask_sb = held.tile([P, BLOCKS, P], F32, name="mask_sb")
+        nc.sync.dma_start(table_sb[:], table)
+        nc.sync.dma_start(offsets[:], offs)
+        nc.scalar.dma_start(w_tok_sb[:], w_tok)
+        nc.scalar.dma_start(w_pos_sb[:], w_pos)
+        nc.sync.dma_start(pos_sb[:], pos)
+        nc.scalar.dma_start(bq_sb[:], bq.rearrange("(a p) o -> p (a o)", p=P))
+        nc.scalar.dma_start(bv_sb[:], bv)
+        nc.scalar.dma_start(bo_sb[:], b_o.rearrange("(h p) o -> p (h o)", p=P))
+        nc.gpsimd.dma_start(w_o_sb[:], w_o.rearrange("(a p) m -> p a m", p=P))
+        for b in reversed(range(BLOCKS)):
+            nc.sync.dma_start(mask_sb[:, b, :], mask[b * P:(b + 1) * P, b * P:(b + 1) * P])
+
+        ident = held.tile([P, P], BF16, name="ident")
+        make_identity(nc, ident[:])
+        bias = held.tile([P, 4], F32, name="bias")
+        nc.vector.memset(bias[:], 0.0)
+        nc.vector.tensor_copy(bias[:, 0:HEADS], bq_sb[:])
+        nc.vector.tensor_copy(bias[:, VAL:VAL + 1], bv_sb[:])
+        penalty = held.tile([P, BLOCKS, P], BF16, name="penalty")
+        for b in reversed(range(BLOCKS)):
+            nc.gpsimd.tensor_scalar(out=penalty[:, b, :], in0=mask_sb[:, b, :], scalar1=-1.0, scalar2=MASKED,
+                                    op0=ALU.add, op1=ALU.mult)
+
+        tok_part = held.tile([P, 4, TOKENS], F32, name="tok_part")
+        for m in range(4):
+            for k in range(PIECES):
+                cols = slice(k * PIECE, (k + 1) * PIECE)
+                g_ps = wide.tile([P, PIECE], F32, name="g_ps", tag="wide")
+                picked = table_sb[:].indirect(offsets[:, k * (PIECE // 16):(k + 1) * (PIECE // 16)])
+                nc.tensor.matmul(g_ps[:], w_tok_sb[:, m * P:(m + 1) * P], picked, start=True, stop=True)
+                if k % 2 == 0:
+                    nc.scalar.activation(out=tok_part[:, m, cols], in_=g_ps[:], func=FUNC.Identity,
+                                         bias=bias[:, m:m + 1])
+                else:
+                    nc.vector.tensor_scalar(out=tok_part[:, m, cols], in0=g_ps[:], scalar1=bias[:, m:m + 1],
+                                            scalar2=None, op0=ALU.add)
+
+        proj = held.tile([P, 4, TOKENS], BF16, name="proj")
+
+        def project(m, k):
+            cols = slice(k * PIECE, (k + 1) * PIECE)
+            p_ps = wide.tile([P, PIECE], F32, name="p_ps", tag="wide")
+            nc.tensor.matmul(p_ps[:], w_pos_sb[:, m * P:(m + 1) * P], pos_sb[:, cols], start=True, stop=True)
+            nc.vector.tensor_tensor(out=proj[:, m, cols], in0=p_ps[:], in1=tok_part[:, m, cols], op=ALU.add)
+
+        val_t = held.tile([P, BLOCKS, VPITCH], BF16, name="val_t")
+
+        def flip_values():
+            nc.vector.memset(val_t[:], 1.0)
+            for k in range(PIECES):
+                project(VAL, k)
+            for b0 in range(0, BLOCKS, FLIPS):
+                v_ps = flip.tile([P, FLIPS * P], BF16, name="v_ps", tag="flip")
+                for i in range(FLIPS):
+                    nc.tensor.transpose(v_ps[:, i * P:(i + 1) * P], proj[:, VAL, (b0 + i) * P:(b0 + i + 1) * P],
+                                        ident[:])
+                nc.vector.tensor_copy(val_t[:, b0:b0 + FLIPS, 0:P], v_ps[:].rearrange("p (b d) -> p b d", b=FLIPS))
+
+        def exponentials(qb, a):
+            keys = (qb + 1) * P
+            chunks = (keys + PIECE - 1) // PIECE
+            neg = rows.tile([P, TOKENS], F32, name="neg")
+            low = small.tile([P, PIECES], F32, name="low")
+            for c in range(chunks):
+                width = min(PIECE, keys - c * PIECE)
+                on_diagonal = c == chunks - 1
+                s_ps = wide.tile([P, PIECE], F32, name="s_ps", tag="wide")
+                nc.tensor.matmul(s_ps[:, :width], proj[:, a, qb * P:(qb + 1) * P],
+                                 proj[:, KEY, c * PIECE:c * PIECE + width], start=True, stop=not on_diagonal)
+                if on_diagonal:
+                    nc.tensor.matmul(s_ps[:, width - P:width], penalty[:, qb, :], ident[:], start=False, stop=True)
+                nc.vector.tensor_scalar(out=neg[:, c * PIECE:c * PIECE + width], in0=s_ps[:, :width],
+                                        scalar1=-SCALE, scalar2=low[:, c - 1:c] if c > 0 else None,
+                                        op0=ALU.mult, op1=ALU.min, accum_out=low[:, c:c + 1])
+            e = rows.tile([P, TOKENS], BF16, name="e")
+            nc.scalar.activation(out=e[:, :keys], in_=neg[:, :keys], func=FUNC.Exp,
+                                 bias=low[:, chunks - 1:chunks], scale=-1.0)
+            return e
+
+        def weighted_sum(qb, a, e, att_q):
+            e_t = rows.tile([P, TOKENS], BF16, name="e_t")
+            for b0 in range(0, qb + 1, FLIPS):
+                n = min(FLIPS, qb + 1 - b0)
+                t_ps = flip.tile([P, FLIPS * P], BF16, name="t_ps", tag="flip")
+                for i in range(n):
+                    nc.tensor.transpose(t_ps[:, i * P:(i + 1) * P], e[:, (b0 + i) * P:(b0 + i + 1) * P], ident[:])
+                if a == 0:
+                    nc.vector.tensor_copy(e_t[:, b0 * P:(b0 + n) * P], t_ps[:, :n * P])
+                else:
+                    nc.scalar.copy(e_t[:, b0 * P:(b0 + n) * P], t_ps[:, :n * P])
+            acc = sums.tile([P, P + 1], F32, name="acc")
+            for b in range(qb + 1):
+                nc.tensor.matmul(acc[:], e_t[:, b * P:(b + 1) * P], val_t[:, b, 0:P + 1],
+                                 start=b == 0, stop=b == qb)
+            inv = small.tile([P, 1], F32, name="inv")
+            nc.vector.reciprocal(inv[:], acc[:, P:P + 1])
+            nc.scalar.activation(out=att_q[:, a, :], in_=acc[:, 0:P], func=FUNC.Copy, scale=inv[:, 0:1])
+
+        out_view = out.rearrange("(h p) j -> p h j", p=P)
+
+        def output(qb, att_q):
+            a_ps = flip.tile([P, FLIPS * P], BF16, name="a_ps", tag="flip")
+            for a in range(HEADS):
+                nc.tensor.transpose(a_ps[:, a * P:(a + 1) * P], att_q[:, a, :], ident[:])
+            att = small.tile([P, HEADS, P], BF16, name="att")
+            nc.vector.tensor_copy(att[:], a_ps[:, :HEADS * P].rearrange("p (a j) -> p a j", a=HEADS))
+            o_ps = wide.tile([P, PIECE], F32, name="o_ps", tag="wide")
+            for h in range(2):
+                for a in range(HEADS):
+                    nc.tensor.matmul(o_ps[:, h * P:(h + 1) * P], w_o_sb[:, a, h * P:(h + 1) * P], att[:, a, :],
+                                     start=a == 0, stop=a == HEADS - 1)
+            o_sb = small.tile([P, 2, P], F32, name="o_sb")
+            nc.vector.tensor_tensor(out=o_sb[:], in0=o_ps[:, :2 * P].rearrange("p (h j) -> p h j", h=2),
+                                    in1=bo_sb[:].unsqueeze(2).to_broadcast([P, 2, P]), op=ALU.add)
+            nc.sync.dma_start(out_view[:, :, qb * P:(qb + 1) * P], o_sb[:])
+
+        for k in range(PIECES):
+            project(KEY, k)
+        order = [(qb, a) for qb in reversed(range(BLOCKS)) for a in range(HEADS)]
+
+        def start_row(qb, a):
+            if a == 0 and qb % (PIECE // P) == PIECE // P - 1:
+                for head in range(HEADS):
+                    project(head, qb // (PIECE // P))
+            return exponentials(qb, a)
+
+        e_next = start_row(*order[0])
+        flip_values()
+        att_q = None
+        for i, (qb, a) in enumerate(order):
+            e_now = e_next
+            if i + 1 < len(order):
+                e_next = start_row(*order[i + 1])
+            if a == 0:
+                att_q = small.tile([P, HEADS, P], BF16, name="att_q")
+            weighted_sum(qb, a, e_now, att_q)
+            if a == HEADS - 1:
+                output(qb, att_q)

@@ -13,10 +13,20 @@ BLOCKS = TOKENS // P
 PIECE = 512
 PIECES = TOKENS // PIECE
 KEY, VAL = HEADS, HEADS + 1
-FLIPS = 8
+PER = PIECE // P
 VPITCH = 136
 SCALE = P ** -0.5
 MASKED = 1.0e9
+LAG_MIN = 2
+LAG_EXP = 6
+LAG_FLIP = LAG_EXP + 2
+LAG_SUM = LAG_FLIP + 2
+LAG_INV = LAG_SUM + 1
+LAG_DIV = LAG_INV + 1
+LAG_ATT = LAG_DIV + 1
+LAG_COPY = LAG_ATT + 1
+LAG_OUT = LAG_COPY + 1
+LAG_STORE = LAG_OUT + 1
 
 PAIRS = TOKENS * (TOKENS + 1) // 2
 FLOPS = 2 * (2 * P) * (4 * P) * TOKENS + HEADS * 2 * (2 * P * PAIRS) + 2 * (2 * P) * (2 * P) * TOKENS
@@ -28,10 +38,10 @@ def tile_mytransformer_b_kernel(tc, table, w_tok, pos, w_pos, bq, bv, mask, w_o,
     nc = tc.nc
     with (
         tc.tile_pool(name="held", bufs=1) as held,
-        tc.tile_pool(name="rows", bufs=3) as rows,
-        tc.tile_pool(name="small", bufs=4) as small,
-        tc.psum_pool(name="wide", bufs=4) as wide,
-        tc.psum_pool(name="flip", bufs=2) as flip,
+        tc.tile_pool(name="chunk", bufs=4) as chunk,
+        tc.tile_pool(name="small", bufs=8) as small,
+        tc.psum_pool(name="wide", bufs=3) as wide,
+        tc.psum_pool(name="flip", bufs=3) as flip,
         tc.psum_pool(name="sums", bufs=2) as sums,
     ):
         table_sb = held.tile([P, WORDS], BF16, name="table_sb")
@@ -44,16 +54,17 @@ def tile_mytransformer_b_kernel(tc, table, w_tok, pos, w_pos, bq, bv, mask, w_o,
         bv_sb = held.tile([P, 1], F32, name="bv_sb")
         bo_sb = held.tile([P, 2], F32, name="bo_sb")
         mask_sb = held.tile([P, BLOCKS, P], F32, name="mask_sb")
-        nc.sync.dma_start(table_sb[:], table)
-        nc.sync.dma_start(offsets[:], offs)
-        nc.scalar.dma_start(w_tok_sb[:], w_tok)
         nc.scalar.dma_start(w_pos_sb[:], w_pos)
-        nc.sync.dma_start(pos_sb[:], pos)
+        for k in range(PIECES):
+            nc.sync.dma_start(pos_sb[:, k * PIECE:(k + 1) * PIECE], pos[:, k * PIECE:(k + 1) * PIECE])
         nc.scalar.dma_start(bq_sb[:], bq.rearrange("(a p) o -> p (a o)", p=P))
         nc.scalar.dma_start(bv_sb[:], bv)
+        nc.sync.dma_start(offsets[:], offs)
+        nc.sync.dma_start(table_sb[:], table)
+        nc.scalar.dma_start(w_tok_sb[:], w_tok)
         nc.scalar.dma_start(bo_sb[:], b_o.rearrange("(h p) o -> p (h o)", p=P))
         nc.gpsimd.dma_start(w_o_sb[:], w_o.rearrange("(a p) m -> p a m", p=P))
-        for b in reversed(range(BLOCKS)):
+        for b in range(BLOCKS):
             nc.sync.dma_start(mask_sb[:, b, :], mask[b * P:(b + 1) * P, b * P:(b + 1) * P])
 
         ident = held.tile([P, P], BF16, name="ident")
@@ -63,122 +74,192 @@ def tile_mytransformer_b_kernel(tc, table, w_tok, pos, w_pos, bq, bv, mask, w_o,
         nc.vector.tensor_copy(bias[:, 0:HEADS], bq_sb[:])
         nc.vector.tensor_copy(bias[:, VAL:VAL + 1], bv_sb[:])
         penalty = held.tile([P, BLOCKS, P], BF16, name="penalty")
-        for b in reversed(range(BLOCKS)):
+        for b in range(BLOCKS):
             nc.gpsimd.tensor_scalar(out=penalty[:, b, :], in0=mask_sb[:, b, :], scalar1=-1.0, scalar2=MASKED,
                                     op0=ALU.add, op1=ALU.mult)
 
-        tok_part = held.tile([P, 4, TOKENS], F32, name="tok_part")
-        for m in range(4):
-            for k in range(PIECES):
+        pos_part = held.tile([P, 4, TOKENS], F32, name="pos_part")
+        for k in range(PIECES):
+            for m in range(4):
+                cols = slice(k * PIECE, (k + 1) * PIECE)
+                p_ps = wide.tile([P, PIECE], F32, name="p_ps", tag="wide")
+                nc.tensor.matmul(p_ps[:], w_pos_sb[:, m * P:(m + 1) * P], pos_sb[:, cols], start=True, stop=True)
+                if m % 2 == 0:
+                    nc.scalar.activation(out=pos_part[:, m, cols], in_=p_ps[:], func=FUNC.Identity,
+                                         bias=bias[:, m:m + 1])
+                else:
+                    nc.vector.tensor_scalar(out=pos_part[:, m, cols], in0=p_ps[:], scalar1=bias[:, m:m + 1],
+                                            scalar2=None, op0=ALU.add)
+
+        proj = held.tile([P, 4, TOKENS], BF16, name="proj")
+        val_t = held.tile([P, BLOCKS, VPITCH], BF16, name="val_t")
+        nc.vector.memset(val_t[:], 1.0)
+
+        def flip_values(k):
+            v_ps = flip.tile([P, PIECE], BF16, name="v_ps", tag="flip")
+            for i in range(PER):
+                nc.tensor.transpose(v_ps[:, i * P:(i + 1) * P], proj[:, VAL, (k * PER + i) * P:(k * PER + i + 1) * P],
+                                    ident[:])
+            nc.scalar.copy(val_t[:, k * PER:(k + 1) * PER, 0:P], v_ps[:].rearrange("p (b d) -> p b d", b=PER))
+
+        for k in range(PIECES):
+            for m in range(4):
                 cols = slice(k * PIECE, (k + 1) * PIECE)
                 g_ps = wide.tile([P, PIECE], F32, name="g_ps", tag="wide")
                 picked = table_sb[:].indirect(offsets[:, k * (PIECE // 16):(k + 1) * (PIECE // 16)])
                 nc.tensor.matmul(g_ps[:], w_tok_sb[:, m * P:(m + 1) * P], picked, start=True, stop=True)
-                if k % 2 == 0:
-                    nc.scalar.activation(out=tok_part[:, m, cols], in_=g_ps[:], func=FUNC.Identity,
-                                         bias=bias[:, m:m + 1])
-                else:
-                    nc.vector.tensor_scalar(out=tok_part[:, m, cols], in0=g_ps[:], scalar1=bias[:, m:m + 1],
-                                            scalar2=None, op0=ALU.add)
+                nc.vector.tensor_tensor(out=proj[:, m, cols], in0=g_ps[:], in1=pos_part[:, m, cols], op=ALU.add)
+            if k > 0:
+                flip_values(k - 1)
 
-        proj = held.tile([P, 4, TOKENS], BF16, name="proj")
+        s_ps, neg, e, t_ps, e_t = {}, {}, {}, {}, {}
+        low, lowest = {}, {}
+        acc, inv, att_q, a_ps, att, o_ps = {}, {}, {}, {}, {}, {}
 
-        def project(m, k):
-            cols = slice(k * PIECE, (k + 1) * PIECE)
-            p_ps = wide.tile([P, PIECE], F32, name="p_ps", tag="wide")
-            nc.tensor.matmul(p_ps[:], w_pos_sb[:, m * P:(m + 1) * P], pos_sb[:, cols], start=True, stop=True)
-            nc.vector.tensor_tensor(out=proj[:, m, cols], in0=p_ps[:], in1=tok_part[:, m, cols], op=ALU.add)
+        def chunks_of(qb):
+            return (qb + PER) // PER
 
-        val_t = held.tile([P, BLOCKS, VPITCH], BF16, name="val_t")
+        def blocks_of(qb, c):
+            return min(PER, qb + 1 - c * PER)
 
-        def flip_values():
-            nc.vector.memset(val_t[:], 1.0)
-            for k in range(PIECES):
-                project(VAL, k)
-            for b0 in range(0, BLOCKS, FLIPS):
-                v_ps = flip.tile([P, FLIPS * P], BF16, name="v_ps", tag="flip")
-                for i in range(FLIPS):
-                    nc.tensor.transpose(v_ps[:, i * P:(i + 1) * P], proj[:, VAL, (b0 + i) * P:(b0 + i + 1) * P],
-                                        ident[:])
-                nc.vector.tensor_copy(val_t[:, b0:b0 + FLIPS, 0:P], v_ps[:].rearrange("p (b d) -> p b d", b=FLIPS))
+        def ends_row(qb, a, c):
+            return c == chunks_of(qb) - 1
 
-        def exponentials(qb, a):
-            keys = (qb + 1) * P
-            chunks = (keys + PIECE - 1) // PIECE
-            neg = rows.tile([P, TOKENS], F32, name="neg")
-            low = small.tile([P, PIECES], F32, name="low")
-            for c in range(chunks):
-                width = min(PIECE, keys - c * PIECE)
-                on_diagonal = c == chunks - 1
-                s_ps = wide.tile([P, PIECE], F32, name="s_ps", tag="wide")
-                nc.tensor.matmul(s_ps[:, :width], proj[:, a, qb * P:(qb + 1) * P],
-                                 proj[:, KEY, c * PIECE:c * PIECE + width], start=True, stop=not on_diagonal)
-                if on_diagonal:
-                    nc.tensor.matmul(s_ps[:, width - P:width], penalty[:, qb, :], ident[:], start=False, stop=True)
-                nc.vector.tensor_scalar(out=neg[:, c * PIECE:c * PIECE + width], in0=s_ps[:, :width],
-                                        scalar1=-SCALE, scalar2=low[:, c - 1:c] if c > 0 else None,
-                                        op0=ALU.mult, op1=ALU.min, accum_out=low[:, c:c + 1])
-            e = rows.tile([P, TOKENS], BF16, name="e")
-            nc.scalar.activation(out=e[:, :keys], in_=neg[:, :keys], func=FUNC.Exp,
-                                 bias=low[:, chunks - 1:chunks], scale=-1.0)
-            return e
+        def ends_block(qb, a, c):
+            return a == HEADS - 1 and c == chunks_of(qb) - 1
 
-        def weighted_sum(qb, a, e, att_q):
-            e_t = rows.tile([P, TOKENS], BF16, name="e_t")
-            for b0 in range(0, qb + 1, FLIPS):
-                n = min(FLIPS, qb + 1 - b0)
-                t_ps = flip.tile([P, FLIPS * P], BF16, name="t_ps", tag="flip")
-                for i in range(n):
-                    nc.tensor.transpose(t_ps[:, i * P:(i + 1) * P], e[:, (b0 + i) * P:(b0 + i + 1) * P], ident[:])
-                if a == 0:
-                    nc.vector.tensor_copy(e_t[:, b0 * P:(b0 + n) * P], t_ps[:, :n * P])
-                else:
-                    nc.scalar.copy(e_t[:, b0 * P:(b0 + n) * P], t_ps[:, :n * P])
-            acc = sums.tile([P, P + 1], F32, name="acc")
-            for b in range(qb + 1):
-                nc.tensor.matmul(acc[:], e_t[:, b * P:(b + 1) * P], val_t[:, b, 0:P + 1],
+        def score_matmuls(qb, a, c):
+            width = blocks_of(qb, c) * P
+            s_ps[qb, a, c] = wide.tile([P, PIECE], F32, name="s_ps", tag="wide")
+            nc.tensor.matmul(s_ps[qb, a, c][:, :width], proj[:, a, qb * P:(qb + 1) * P],
+                             proj[:, KEY, c * PIECE:c * PIECE + width], start=True, stop=not ends_row(qb, a, c))
+            if ends_row(qb, a, c):
+                nc.tensor.matmul(s_ps[qb, a, c][:, width - P:width], penalty[:, qb, :], ident[:],
+                                 start=False, stop=True)
+
+        def scores_out(qb, a, c):
+            if c == 0:
+                low[qb, a] = small.tile([P, PIECES], F32, name="low")
+            width = blocks_of(qb, c) * P
+            neg[qb, a, c] = chunk.tile([P, PIECE], F32, name="neg", bufs=LAG_EXP + 2)
+            nc.vector.tensor_scalar(out=neg[qb, a, c][:, :width], in0=s_ps[qb, a, c][:, :width], scalar1=-SCALE,
+                                    scalar2=None, op0=ALU.mult, op1=ALU.min, accum_out=low[qb, a][:, c:c + 1])
+
+        def row_minimum(qb, a):
+            lowest[qb, a] = small.tile([P, 1], F32, name="lowest")
+            nc.vector.tensor_reduce(out=lowest[qb, a][:], in_=low[qb, a][:, :chunks_of(qb)],
+                                    axis=mybir.AxisListType.X, op=ALU.min)
+
+        def exponentials(qb, a, c):
+            width = blocks_of(qb, c) * P
+            e[qb, a, c] = chunk.tile([P, PIECE], BF16, name="e")
+            nc.scalar.activation(out=e[qb, a, c][:, :width], in_=neg[qb, a, c][:, :width], func=FUNC.Exp,
+                                 bias=lowest[qb, a][:, 0:1], scale=-1.0)
+
+        def flips(qb, a, c):
+            t_ps[qb, a, c] = flip.tile([P, PIECE], BF16, name="t_ps", tag="flip")
+            for i in range(blocks_of(qb, c)):
+                nc.tensor.transpose(t_ps[qb, a, c][:, i * P:(i + 1) * P], e[qb, a, c][:, i * P:(i + 1) * P], ident[:])
+
+        def flips_out(qb, a, c, by_scalar):
+            width = blocks_of(qb, c) * P
+            e_t[qb, a, c] = chunk.tile([P, PIECE], BF16, name="e_t")
+            if by_scalar:
+                nc.scalar.copy(e_t[qb, a, c][:, :width], t_ps[qb, a, c][:, :width])
+            else:
+                nc.vector.tensor_copy(e_t[qb, a, c][:, :width], t_ps[qb, a, c][:, :width])
+
+        def weighted_sum(qb, a, c):
+            if a == 0 and c == 0:
+                acc[qb] = sums.tile([P, HEADS, VPITCH], F32, name="acc")
+            for i in range(blocks_of(qb, c)):
+                b = c * PER + i
+                nc.tensor.matmul(acc[qb][:, a, 0:P + 1], e_t[qb, a, c][:, i * P:(i + 1) * P], val_t[:, b, 0:P + 1],
                                  start=b == 0, stop=b == qb)
-            inv = small.tile([P, 1], F32, name="inv")
-            nc.vector.reciprocal(inv[:], acc[:, P:P + 1])
-            nc.scalar.activation(out=att_q[:, a, :], in_=acc[:, 0:P], func=FUNC.Copy, scale=inv[:, 0:1])
+
+        def reciprocals(qb):
+            inv[qb] = small.tile([P, HEADS, 1], F32, name="inv")
+            nc.vector.reciprocal(inv[qb][:], acc[qb][:, :, P:P + 1])
+
+        def divide(qb):
+            att_q[qb] = small.tile([P, HEADS, P], BF16, name="att_q")
+            for a in range(HEADS):
+                nc.scalar.activation(out=att_q[qb][:, a, :], in_=acc[qb][:, a, 0:P], func=FUNC.Copy,
+                                     scale=inv[qb][:, a, :])
+
+        def att_flips(qb):
+            a_ps[qb] = flip.tile([P, PIECE], BF16, name="a_ps", tag="flip")
+            for a in range(HEADS):
+                nc.tensor.transpose(a_ps[qb][:, a * P:(a + 1) * P], att_q[qb][:, a, :], ident[:])
+
+        def att_out(qb):
+            att[qb] = small.tile([P, HEADS * P], BF16, name="att")
+            nc.vector.tensor_copy(att[qb][:], a_ps[qb][:, :HEADS * P])
+
+        def output_matmuls(qb):
+            o_ps[qb] = wide.tile([P, PIECE], F32, name="o_ps", tag="wide")
+            for h in range(2):
+                for a in range(HEADS):
+                    nc.tensor.matmul(o_ps[qb][:, h * P:(h + 1) * P], w_o_sb[:, a, h * P:(h + 1) * P],
+                                     att[qb][:, a * P:(a + 1) * P], start=a == 0, stop=a == HEADS - 1)
 
         out_view = out.rearrange("(h p) j -> p h j", p=P)
 
-        def output(qb, att_q):
-            a_ps = flip.tile([P, FLIPS * P], BF16, name="a_ps", tag="flip")
-            for a in range(HEADS):
-                nc.tensor.transpose(a_ps[:, a * P:(a + 1) * P], att_q[:, a, :], ident[:])
-            att = small.tile([P, HEADS, P], BF16, name="att")
-            nc.vector.tensor_copy(att[:], a_ps[:, :HEADS * P].rearrange("p (a j) -> p a j", a=HEADS))
-            o_ps = wide.tile([P, PIECE], F32, name="o_ps", tag="wide")
-            for h in range(2):
-                for a in range(HEADS):
-                    nc.tensor.matmul(o_ps[:, h * P:(h + 1) * P], w_o_sb[:, a, h * P:(h + 1) * P], att[:, a, :],
-                                     start=a == 0, stop=a == HEADS - 1)
+        def store(qb):
             o_sb = small.tile([P, 2, P], F32, name="o_sb")
-            nc.vector.tensor_tensor(out=o_sb[:], in0=o_ps[:, :2 * P].rearrange("p (h j) -> p h j", h=2),
-                                    in1=bo_sb[:].unsqueeze(2).to_broadcast([P, 2, P]), op=ALU.add)
+            for h in range(2):
+                nc.scalar.activation(out=o_sb[:, h, :], in_=o_ps[qb][:, h * P:(h + 1) * P], func=FUNC.Identity,
+                                     bias=bo_sb[:, h:h + 1])
             nc.sync.dma_start(out_view[:, :, qb * P:(qb + 1) * P], o_sb[:])
 
-        for k in range(PIECES):
-            project(KEY, k)
-        order = [(qb, a) for qb in reversed(range(BLOCKS)) for a in range(HEADS)]
+        block_order = list(range(1, BLOCKS, 2)) + list(reversed(range(0, BLOCKS, 2)))
+        belt = [(qb, a, c) for qb in block_order for a in range(HEADS) for c in range(chunks_of(qb))]
 
-        def start_row(qb, a):
-            if a == 0 and qb % (PIECE // P) == PIECE // P - 1:
-                for head in range(HEADS):
-                    project(head, qb // (PIECE // P))
-            return exponentials(qb, a)
+        def due(t, lag, only=None):
+            if not 0 <= t - lag < len(belt):
+                return None
+            x = belt[t - lag]
+            return x if only is None or only(*x) else None
 
-        e_next = start_row(*order[0])
-        flip_values()
-        att_q = None
-        for i, (qb, a) in enumerate(order):
-            e_now = e_next
-            if i + 1 < len(order):
-                e_next = start_row(*order[i + 1])
-            if a == 0:
-                att_q = small.tile([P, HEADS, P], BF16, name="att_q")
-            weighted_sum(qb, a, e_now, att_q)
-            if a == HEADS - 1:
-                output(qb, att_q)
+        for t in range(len(belt) + LAG_STORE + 1):
+            x = due(t, 0)
+            if x:
+                score_matmuls(*x)
+            x = due(t, LAG_EXP)
+            if x:
+                exponentials(*x)
+            x = due(t, LAG_MIN, ends_row)
+            if x:
+                row_minimum(x[0], x[1])
+            x = due(t, LAG_INV, ends_block)
+            if x:
+                reciprocals(x[0])
+            x = due(t, LAG_DIV, ends_block)
+            if x:
+                divide(x[0])
+            x = due(t, LAG_COPY, ends_block)
+            if x:
+                att_out(x[0])
+            x = due(t, LAG_STORE, ends_block)
+            if x:
+                store(x[0])
+            x = due(t, LAG_FLIP)
+            if x:
+                flips(*x)
+            x = due(t, LAG_SUM)
+            if x:
+                weighted_sum(*x)
+            if t == 2:
+                flip_values(PIECES - 1)
+            x = due(t, LAG_ATT, ends_block)
+            if x:
+                att_flips(x[0])
+            x = due(t, LAG_OUT, ends_block)
+            if x:
+                output_matmuls(x[0])
+            x = due(t, 0)
+            if x:
+                scores_out(*x)
+            x = due(t, LAG_FLIP)
+            if x:
+                flips_out(*x, t % 4 == 3)

@@ -19,13 +19,14 @@ SCALE = P ** -0.5
 MASKED = 1.0e9
 LAG_MIN = 2
 LAG_EXP = 6
-LAG_FLIP = LAG_EXP + 2
-LAG_SUM = LAG_FLIP + 2
+AHEAD = 4
+LAG_FLIP = LAG_EXP + AHEAD
+LAG_SUM = LAG_FLIP + AHEAD
 LAG_INV = LAG_SUM + 1
 LAG_DIV = LAG_INV + 1
-LAG_ATT = LAG_DIV + 1
+LAG_ATT = LAG_DIV + AHEAD
 LAG_COPY = LAG_ATT + 1
-LAG_OUT = LAG_COPY + 1
+LAG_OUT = LAG_COPY + AHEAD
 LAG_STORE = LAG_OUT + 1
 
 PAIRS = TOKENS * (TOKENS + 1) // 2
@@ -152,7 +153,7 @@ def tile_mytransformer_b_kernel(tc, table, w_tok, pos, w_pos, bq, bv, mask, w_o,
 
         def exponentials(qb, a, c):
             width = blocks_of(qb, c) * P
-            e[qb, a, c] = chunk.tile([P, PIECE], BF16, name="e")
+            e[qb, a, c] = chunk.tile([P, PIECE], BF16, name="e", bufs=AHEAD + 2)
             nc.scalar.activation(out=e[qb, a, c][:, :width], in_=neg[qb, a, c][:, :width], func=FUNC.Exp,
                                  bias=lowest[qb, a][:, 0:1], scale=-1.0)
 
@@ -163,7 +164,7 @@ def tile_mytransformer_b_kernel(tc, table, w_tok, pos, w_pos, bq, bv, mask, w_o,
 
         def flips_out(qb, a, c, by_scalar):
             width = blocks_of(qb, c) * P
-            e_t[qb, a, c] = chunk.tile([P, PIECE], BF16, name="e_t")
+            e_t[qb, a, c] = chunk.tile([P, PIECE], BF16, name="e_t", bufs=AHEAD + 2)
             if by_scalar:
                 nc.scalar.copy(e_t[qb, a, c][:, :width], t_ps[qb, a, c][:, :width])
             else:
@@ -222,9 +223,6 @@ def tile_mytransformer_b_kernel(tc, table, w_tok, pos, w_pos, bq, bv, mask, w_o,
             return x if only is None or only(*x) else None
 
         for t in range(len(belt) + LAG_STORE + 1):
-            x = due(t, 0)
-            if x:
-                score_matmuls(*x)
             x = due(t, LAG_EXP)
             if x:
                 exponentials(*x)
@@ -259,6 +257,7 @@ def tile_mytransformer_b_kernel(tc, table, w_tok, pos, w_pos, bq, bv, mask, w_o,
                 output_matmuls(x[0])
             x = due(t, 0)
             if x:
+                score_matmuls(*x)
                 scores_out(*x)
             x = due(t, LAG_FLIP)
             if x:

@@ -261,4 +261,4 @@ def tile_mytransformer_b_kernel(tc, table, w_tok, pos, w_pos, bq, bv, mask, w_o,
                 scores_out(*x)
             x = due(t, LAG_FLIP)
             if x:
-                flips_out(*x, t % 4 == 3)
+                flips_out(*x, t % 2 == 1)

@@ -17,9 +17,10 @@ PER = PIECE // P
 VPITCH = 136
 SCALE = P ** -0.5
 MASKED = 1.0e9
-LAG_MIN = 2
-LAG_EXP = 6
-AHEAD = 4
+SPAN = 8
+LAG_MIN = 1
+LAG_EXP = 3
+AHEAD = 3
 LAG_FLIP = LAG_EXP + AHEAD
 LAG_SUM = LAG_FLIP + AHEAD
 LAG_INV = LAG_SUM + 1
@@ -39,10 +40,10 @@ def tile_mytransformer_b_kernel(tc, table, w_tok, pos, w_pos, bq, bv, mask, w_o,
     nc = tc.nc
     with (
         tc.tile_pool(name="held", bufs=1) as held,
-        tc.tile_pool(name="chunk", bufs=4) as chunk,
+        tc.tile_pool(name="span", bufs=4) as span,
         tc.tile_pool(name="small", bufs=8) as small,
-        tc.psum_pool(name="wide", bufs=3) as wide,
-        tc.psum_pool(name="flip", bufs=3) as flip,
+        tc.psum_pool(name="wide", bufs=4) as wide,
+        tc.psum_pool(name="flip", bufs=2) as flip,
         tc.psum_pool(name="sums", bufs=2) as sums,
     ):
         table_sb = held.tile([P, WORDS], BF16, name="table_sb")
@@ -117,65 +118,71 @@ def tile_mytransformer_b_kernel(tc, table, w_tok, pos, w_pos, bq, bv, mask, w_o,
         low, lowest = {}, {}
         acc, inv, att_q, a_ps, att, o_ps = {}, {}, {}, {}, {}, {}
 
-        def chunks_of(qb):
-            return (qb + PER) // PER
+        def spans_of(qb):
+            return (qb + SPAN) // SPAN
 
-        def blocks_of(qb, c):
-            return min(PER, qb + 1 - c * PER)
+        def blocks_of(qb, s):
+            return min(SPAN, qb + 1 - s * SPAN)
 
-        def ends_row(qb, a, c):
-            return c == chunks_of(qb) - 1
+        def halves_of(qb, s):
+            n = blocks_of(qb, s)
+            return [(h, s * SPAN + h * PER, min(PER, n - h * PER) * P) for h in range((n + PER - 1) // PER)]
 
-        def ends_block(qb, a, c):
-            return a == HEADS - 1 and c == chunks_of(qb) - 1
+        def ends_row(qb, a, s):
+            return s == spans_of(qb) - 1
 
-        def score_matmuls(qb, a, c):
-            width = blocks_of(qb, c) * P
-            s_ps[qb, a, c] = wide.tile([P, PIECE], F32, name="s_ps", tag="wide")
-            nc.tensor.matmul(s_ps[qb, a, c][:, :width], proj[:, a, qb * P:(qb + 1) * P],
-                             proj[:, KEY, c * PIECE:c * PIECE + width], start=True, stop=not ends_row(qb, a, c))
-            if ends_row(qb, a, c):
-                nc.tensor.matmul(s_ps[qb, a, c][:, width - P:width], penalty[:, qb, :], ident[:],
-                                 start=False, stop=True)
+        def ends_block(qb, a, s):
+            return a == HEADS - 1 and s == spans_of(qb) - 1
 
-        def scores_out(qb, a, c):
-            if c == 0:
+        def score_matmuls(qb, a, s):
+            for h, b0, width in halves_of(qb, s):
+                on_diagonal = b0 * P + width == (qb + 1) * P
+                s_ps[qb, a, s, h] = wide.tile([P, PIECE], F32, name="s_ps", tag="wide")
+                nc.tensor.matmul(s_ps[qb, a, s, h][:, :width], proj[:, a, qb * P:(qb + 1) * P],
+                                 proj[:, KEY, b0 * P:b0 * P + width], start=True, stop=not on_diagonal)
+                if on_diagonal:
+                    nc.tensor.matmul(s_ps[qb, a, s, h][:, width - P:width], penalty[:, qb, :], ident[:],
+                                     start=False, stop=True)
+
+        def scores_out(qb, a, s):
+            if s == 0:
                 low[qb, a] = small.tile([P, PIECES], F32, name="low")
-            width = blocks_of(qb, c) * P
-            neg[qb, a, c] = chunk.tile([P, PIECE], F32, name="neg", bufs=LAG_EXP + 2)
-            nc.vector.tensor_scalar(out=neg[qb, a, c][:, :width], in0=s_ps[qb, a, c][:, :width], scalar1=-SCALE,
-                                    scalar2=None, op0=ALU.mult, op1=ALU.min, accum_out=low[qb, a][:, c:c + 1])
+            neg[qb, a, s] = span.tile([P, SPAN * P], F32, name="neg", bufs=LAG_EXP + 2)
+            for h, b0, width in halves_of(qb, s):
+                nc.vector.tensor_scalar(out=neg[qb, a, s][:, h * PIECE:h * PIECE + width],
+                                        in0=s_ps[qb, a, s, h][:, :width], scalar1=-SCALE, scalar2=None,
+                                        op0=ALU.mult, op1=ALU.min, accum_out=low[qb, a][:, b0 // PER:b0 // PER + 1])
 
         def row_minimum(qb, a):
             lowest[qb, a] = small.tile([P, 1], F32, name="lowest")
-            nc.vector.tensor_reduce(out=lowest[qb, a][:], in_=low[qb, a][:, :chunks_of(qb)],
+            nc.vector.tensor_reduce(out=lowest[qb, a][:], in_=low[qb, a][:, :(qb + PER) // PER],
                                     axis=mybir.AxisListType.X, op=ALU.min)
 
-        def exponentials(qb, a, c):
-            width = blocks_of(qb, c) * P
-            e[qb, a, c] = chunk.tile([P, PIECE], BF16, name="e", bufs=AHEAD + 2)
-            nc.scalar.activation(out=e[qb, a, c][:, :width], in_=neg[qb, a, c][:, :width], func=FUNC.Exp,
+        def exponentials(qb, a, s):
+            width = blocks_of(qb, s) * P
+            e[qb, a, s] = span.tile([P, SPAN * P], BF16, name="e", bufs=AHEAD + 2)
+            nc.scalar.activation(out=e[qb, a, s][:, :width], in_=neg[qb, a, s][:, :width], func=FUNC.Exp,
                                  bias=lowest[qb, a][:, 0:1], scale=-1.0)
 
-        def flips(qb, a, c):
-            t_ps[qb, a, c] = flip.tile([P, PIECE], BF16, name="t_ps", tag="flip")
-            for i in range(blocks_of(qb, c)):
-                nc.tensor.transpose(t_ps[qb, a, c][:, i * P:(i + 1) * P], e[qb, a, c][:, i * P:(i + 1) * P], ident[:])
+        def flips(qb, a, s):
+            t_ps[qb, a, s] = flip.tile([P, SPAN * P], BF16, name="t_ps", tag="flip")
+            for i in range(blocks_of(qb, s)):
+                nc.tensor.transpose(t_ps[qb, a, s][:, i * P:(i + 1) * P], e[qb, a, s][:, i * P:(i + 1) * P], ident[:])
 
-        def flips_out(qb, a, c, by_scalar):
-            width = blocks_of(qb, c) * P
-            e_t[qb, a, c] = chunk.tile([P, PIECE], BF16, name="e_t", bufs=AHEAD + 2)
+        def flips_out(qb, a, s, by_scalar):
+            width = blocks_of(qb, s) * P
+            e_t[qb, a, s] = span.tile([P, SPAN * P], BF16, name="e_t", bufs=AHEAD + 2)
             if by_scalar:
-                nc.scalar.copy(e_t[qb, a, c][:, :width], t_ps[qb, a, c][:, :width])
+                nc.scalar.copy(e_t[qb, a, s][:, :width], t_ps[qb, a, s][:, :width])
             else:
-                nc.vector.tensor_copy(e_t[qb, a, c][:, :width], t_ps[qb, a, c][:, :width])
+                nc.vector.tensor_copy(e_t[qb, a, s][:, :width], t_ps[qb, a, s][:, :width])
 
-        def weighted_sum(qb, a, c):
-            if a == 0 and c == 0:
+        def weighted_sum(qb, a, s):
+            if a == 0 and s == 0:
                 acc[qb] = sums.tile([P, HEADS, VPITCH], F32, name="acc")
-            for i in range(blocks_of(qb, c)):
-                b = c * PER + i
-                nc.tensor.matmul(acc[qb][:, a, 0:P + 1], e_t[qb, a, c][:, i * P:(i + 1) * P], val_t[:, b, 0:P + 1],
+            for i in range(blocks_of(qb, s)):
+                b = s * SPAN + i
+                nc.tensor.matmul(acc[qb][:, a, 0:P + 1], e_t[qb, a, s][:, i * P:(i + 1) * P], val_t[:, b, 0:P + 1],
                                  start=b == 0, stop=b == qb)
 
         def reciprocals(qb):
@@ -189,7 +196,7 @@ def tile_mytransformer_b_kernel(tc, table, w_tok, pos, w_pos, bq, bv, mask, w_o,
                                      scale=inv[qb][:, a, :])
 
         def att_flips(qb):
-            a_ps[qb] = flip.tile([P, PIECE], BF16, name="a_ps", tag="flip")
+            a_ps[qb] = wide.tile([P, PIECE], BF16, name="a_ps", tag="wide")
             for a in range(HEADS):
                 nc.tensor.transpose(a_ps[qb][:, a * P:(a + 1) * P], att_q[qb][:, a, :], ident[:])
 
@@ -214,7 +221,7 @@ def tile_mytransformer_b_kernel(tc, table, w_tok, pos, w_pos, bq, bv, mask, w_o,
             nc.sync.dma_start(out_view[:, :, qb * P:(qb + 1) * P], o_sb[:])
 
         block_order = list(range(1, BLOCKS, 2)) + list(reversed(range(0, BLOCKS, 2)))
-        belt = [(qb, a, c) for qb in block_order for a in range(HEADS) for c in range(chunks_of(qb))]
+        belt = [(qb, a, s) for qb in block_order for a in range(HEADS) for s in range(spans_of(qb))]
 
         def due(t, lag, only=None):
             if not 0 <= t - lag < len(belt):
@@ -247,7 +254,7 @@ def tile_mytransformer_b_kernel(tc, table, w_tok, pos, w_pos, bq, bv, mask, w_o,
             x = due(t, LAG_SUM)
             if x:
                 weighted_sum(*x)
-            if t == 2:
+            if t == 1:
                 flip_values(PIECES - 1)
             x = due(t, LAG_ATT, ends_block)
             if x:

@@ -29,6 +29,10 @@ LAG_ATT = LAG_DIV + AHEAD
 LAG_COPY = LAG_ATT + 1
 LAG_OUT = LAG_COPY + AHEAD
 LAG_STORE = LAG_OUT + 1
+EARLY = 2
+UNIT = 2
+FIRST_UNIT = 9
+UNIT_EVERY = 3
 
 PAIRS = TOKENS * (TOKENS + 1) // 2
 FLOPS = 2 * (2 * P) * (4 * P) * TOKENS + HEADS * 2 * (2 * P * PAIRS) + 2 * (2 * P) * (2 * P) * TOKENS
@@ -38,6 +42,7 @@ BYTES = (2 * (P * WORDS + 2 * P * 4 * P + P * TOKENS + 4 * P * P) + 4 * (5 * P) 
 
 def tile_mytransformer_b_kernel(tc, table, w_tok, pos, w_pos, bq, bv, mask, w_o, b_o, offs, out):
     nc = tc.nc
+    block_order = [1, 3, 5, 7, 6, 4, 2, 0, 9, 11, 13, 15, 14, 12, 10, 8]
     with (
         tc.tile_pool(name="held", bufs=1) as held,
         tc.tile_pool(name="span", bufs=4) as span,
@@ -56,17 +61,23 @@ def tile_mytransformer_b_kernel(tc, table, w_tok, pos, w_pos, bq, bv, mask, w_o,
         bv_sb = held.tile([P, 1], F32, name="bv_sb")
         bo_sb = held.tile([P, 2], F32, name="bo_sb")
         mask_sb = held.tile([P, BLOCKS, P], F32, name="mask_sb")
-        nc.scalar.dma_start(w_pos_sb[:], w_pos)
-        for k in range(PIECES):
+
+        def load_pos(k):
             nc.sync.dma_start(pos_sb[:, k * PIECE:(k + 1) * PIECE], pos[:, k * PIECE:(k + 1) * PIECE])
-        nc.scalar.dma_start(bq_sb[:], bq.rearrange("(a p) o -> p (a o)", p=P))
-        nc.scalar.dma_start(bv_sb[:], bv)
+
+        nc.scalar.dma_start(w_pos_sb[:], w_pos)
+        for k in range(EARLY):
+            load_pos(k)
         nc.sync.dma_start(offsets[:], offs)
         nc.sync.dma_start(table_sb[:], table)
         nc.scalar.dma_start(w_tok_sb[:], w_tok)
+        nc.scalar.dma_start(bq_sb[:], bq.rearrange("(a p) o -> p (a o)", p=P))
+        nc.scalar.dma_start(bv_sb[:], bv)
+        for k in range(EARLY, PIECES):
+            load_pos(k)
         nc.scalar.dma_start(bo_sb[:], b_o.rearrange("(h p) o -> p (h o)", p=P))
         nc.gpsimd.dma_start(w_o_sb[:], w_o.rearrange("(a p) m -> p a m", p=P))
-        for b in range(BLOCKS):
+        for b in block_order:
             nc.sync.dma_start(mask_sb[:, b, :], mask[b * P:(b + 1) * P, b * P:(b + 1) * P])
 
         ident = held.tile([P, P], BF16, name="ident")
@@ -76,26 +87,32 @@ def tile_mytransformer_b_kernel(tc, table, w_tok, pos, w_pos, bq, bv, mask, w_o,
         nc.vector.tensor_copy(bias[:, 0:HEADS], bq_sb[:])
         nc.vector.tensor_copy(bias[:, VAL:VAL + 1], bv_sb[:])
         penalty = held.tile([P, BLOCKS, P], BF16, name="penalty")
-        for b in range(BLOCKS):
+        for b in block_order:
             nc.gpsimd.tensor_scalar(out=penalty[:, b, :], in0=mask_sb[:, b, :], scalar1=-1.0, scalar2=MASKED,
                                     op0=ALU.add, op1=ALU.mult)
-
-        pos_part = held.tile([P, 4, TOKENS], F32, name="pos_part")
-        for k in range(PIECES):
-            for m in range(4):
-                cols = slice(k * PIECE, (k + 1) * PIECE)
-                p_ps = wide.tile([P, PIECE], F32, name="p_ps", tag="wide")
-                nc.tensor.matmul(p_ps[:], w_pos_sb[:, m * P:(m + 1) * P], pos_sb[:, cols], start=True, stop=True)
-                if m % 2 == 0:
-                    nc.scalar.activation(out=pos_part[:, m, cols], in_=p_ps[:], func=FUNC.Identity,
-                                         bias=bias[:, m:m + 1])
-                else:
-                    nc.vector.tensor_scalar(out=pos_part[:, m, cols], in0=p_ps[:], scalar1=bias[:, m:m + 1],
-                                            scalar2=None, op0=ALU.add)
 
         proj = held.tile([P, 4, TOKENS], BF16, name="proj")
         val_t = held.tile([P, BLOCKS, VPITCH], BF16, name="val_t")
         nc.vector.memset(val_t[:], 1.0)
+        p_ps = {}
+
+        def project_open(k, m, pool, tag):
+            p_ps[k, m] = pool.tile([P, PIECE], F32, name="p_ps", tag=tag)
+            nc.tensor.matmul(p_ps[k, m][:], w_pos_sb[:, m * P:(m + 1) * P], pos_sb[:, k * PIECE:(k + 1) * PIECE],
+                             start=True, stop=False)
+
+        def project_close(k, m):
+            picked = table_sb[:].indirect(offsets[:, k * (PIECE // 16):(k + 1) * (PIECE // 16)])
+            nc.tensor.matmul(p_ps[k, m][:], w_tok_sb[:, m * P:(m + 1) * P], picked, start=False, stop=True)
+
+        def project_out(k, m):
+            cols = slice(k * PIECE, (k + 1) * PIECE)
+            if m % 2 == 0:
+                nc.scalar.activation(out=proj[:, m, cols], in_=p_ps[k, m][:], func=FUNC.Identity,
+                                     bias=bias[:, m:m + 1])
+            else:
+                nc.vector.tensor_scalar(out=proj[:, m, cols], in0=p_ps[k, m][:], scalar1=bias[:, m:m + 1],
+                                        scalar2=None, op0=ALU.add)
 
         def flip_values(k):
             v_ps = flip.tile([P, PIECE], BF16, name="v_ps", tag="flip")
@@ -104,15 +121,14 @@ def tile_mytransformer_b_kernel(tc, table, w_tok, pos, w_pos, bq, bv, mask, w_o,
                                     ident[:])
             nc.scalar.copy(val_t[:, k * PER:(k + 1) * PER, 0:P], v_ps[:].rearrange("p (b d) -> p b d", b=PER))
 
-        for k in range(PIECES):
+        for m in range(4):
+            project_open(0, m, wide, "wide")
+        for m in range(4):
+            project_open(1, m, flip if m < 2 else sums, "flip" if m < 2 else "acc")
+        for k in range(EARLY):
             for m in range(4):
-                cols = slice(k * PIECE, (k + 1) * PIECE)
-                g_ps = wide.tile([P, PIECE], F32, name="g_ps", tag="wide")
-                picked = table_sb[:].indirect(offsets[:, k * (PIECE // 16):(k + 1) * (PIECE // 16)])
-                nc.tensor.matmul(g_ps[:], w_tok_sb[:, m * P:(m + 1) * P], picked, start=True, stop=True)
-                nc.vector.tensor_tensor(out=proj[:, m, cols], in0=g_ps[:], in1=pos_part[:, m, cols], op=ALU.add)
-            if k > 0:
-                flip_values(k - 1)
+                project_close(k, m)
+                project_out(k, m)
 
         s_ps, neg, e, t_ps, e_t = {}, {}, {}, {}, {}
         low, lowest = {}, {}
@@ -220,14 +236,26 @@ def tile_mytransformer_b_kernel(tc, table, w_tok, pos, w_pos, bq, bv, mask, w_o,
                                      bias=bo_sb[:, h:h + 1])
             nc.sync.dma_start(out_view[:, :, qb * P:(qb + 1) * P], o_sb[:])
 
-        block_order = list(range(1, BLOCKS, 2)) + list(reversed(range(0, BLOCKS, 2)))
-        belt = [(qb, a, s) for qb in block_order for a in range(HEADS) for s in range(spans_of(qb))]
+        units = [(k, m) for k in range(EARLY, PIECES) for m in range(0, 4, UNIT)]
+        belt = []
+        for r, (qb, a) in enumerate([(qb, a) for qb in block_order for a in range(HEADS)]):
+            i, rest = divmod(r - FIRST_UNIT, UNIT_EVERY)
+            if rest == 0 and 0 <= i < len(units):
+                belt.append(units[i])
+            belt.extend([(qb, a, s) for s in range(spans_of(qb))])
 
         def due(t, lag, only=None):
-            if not 0 <= t - lag < len(belt):
+            if not 0 <= t - lag < len(belt) or len(belt[t - lag]) != 3:
                 return None
             x = belt[t - lag]
             return x if only is None or only(*x) else None
+
+        def values_due(t):
+            if 1 <= t <= EARLY:
+                return t - 1
+            if 0 <= t - AHEAD < len(belt) and len(belt[t - AHEAD]) == 2 and belt[t - AHEAD][1] + UNIT == 4:
+                return belt[t - AHEAD][0]
+            return None
 
         for t in range(len(belt) + LAG_STORE + 1):
             x = due(t, LAG_EXP)
@@ -254,8 +282,9 @@ def tile_mytransformer_b_kernel(tc, table, w_tok, pos, w_pos, bq, bv, mask, w_o,
             x = due(t, LAG_SUM)
             if x:
                 weighted_sum(*x)
-            if t == 1:
-                flip_values(PIECES - 1)
+            k = values_due(t)
+            if k is not None:
+                flip_values(k)
             x = due(t, LAG_ATT, ends_block)
             if x:
                 att_flips(x[0])
@@ -266,6 +295,14 @@ def tile_mytransformer_b_kernel(tc, table, w_tok, pos, w_pos, bq, bv, mask, w_o,
             if x:
                 score_matmuls(*x)
                 scores_out(*x)
+            if t < len(belt) and len(belt[t]) == 2:
+                k, m = belt[t]
+                for i in range(UNIT):
+                    project_open(k, m + i, wide, "wide")
+                for i in range(UNIT):
+                    project_close(k, m + i)
+                for i in range(UNIT):
+                    project_out(k, m + i)
             x = due(t, LAG_FLIP)
             if x:
                 flips_out(*x, t % 2 == 1)

@@ -65,12 +65,13 @@ def tile_mytransformer_b_kernel(tc, table, w_tok, pos, w_pos, bq, bv, mask, w_o,
         def load_pos(k):
             nc.sync.dma_start(pos_sb[:, k * PIECE:(k + 1) * PIECE], pos[:, k * PIECE:(k + 1) * PIECE])
 
+        nc.sync.dma_start(offsets[:], offs)
+        nc.scalar.dma_start(w_tok_sb[:], w_tok)
+        nc.sync.dma_start(table_sb[:, :WORDS // 2], table[:, :WORDS // 2])
+        nc.scalar.dma_start(table_sb[:, WORDS // 2:], table[:, WORDS // 2:])
         nc.scalar.dma_start(w_pos_sb[:], w_pos)
         for k in range(EARLY):
             load_pos(k)
-        nc.sync.dma_start(offsets[:], offs)
-        nc.sync.dma_start(table_sb[:], table)
-        nc.scalar.dma_start(w_tok_sb[:], w_tok)
         nc.scalar.dma_start(bq_sb[:], bq.rearrange("(a p) o -> p (a o)", p=P))
         nc.scalar.dma_start(bv_sb[:], bv)
         for k in range(EARLY, PIECES):
@@ -96,14 +97,13 @@ def tile_mytransformer_b_kernel(tc, table, w_tok, pos, w_pos, bq, bv, mask, w_o,
         nc.vector.memset(val_t[:], 1.0)
         p_ps = {}
 
-        def project_open(k, m, pool, tag):
-            p_ps[k, m] = pool.tile([P, PIECE], F32, name="p_ps", tag=tag)
+        def position_part(k, m, first):
             nc.tensor.matmul(p_ps[k, m][:], w_pos_sb[:, m * P:(m + 1) * P], pos_sb[:, k * PIECE:(k + 1) * PIECE],
-                             start=True, stop=False)
+                             start=first, stop=not first)
 
-        def project_close(k, m):
+        def token_part(k, m, first):
             picked = table_sb[:].indirect(offsets[:, k * (PIECE // 16):(k + 1) * (PIECE // 16)])
-            nc.tensor.matmul(p_ps[k, m][:], w_tok_sb[:, m * P:(m + 1) * P], picked, start=False, stop=True)
+            nc.tensor.matmul(p_ps[k, m][:], w_tok_sb[:, m * P:(m + 1) * P], picked, start=first, stop=not first)
 
         def project_out(k, m):
             cols = slice(k * PIECE, (k + 1) * PIECE)
@@ -122,12 +122,16 @@ def tile_mytransformer_b_kernel(tc, table, w_tok, pos, w_pos, bq, bv, mask, w_o,
             nc.scalar.copy(val_t[:, k * PER:(k + 1) * PER, 0:P], v_ps[:].rearrange("p (b d) -> p b d", b=PER))
 
         for m in range(4):
-            project_open(0, m, wide, "wide")
-        for m in range(4):
-            project_open(1, m, flip if m < 2 else sums, "flip" if m < 2 else "acc")
+            p_ps[0, m] = wide.tile([P, PIECE], F32, name="p_ps", tag="wide")
+        for m in range(2):
+            p_ps[1, m] = flip.tile([P, PIECE], F32, name="p_ps", tag="flip")
+            p_ps[1, m + 2] = sums.tile([P, PIECE], F32, name="p_ps", tag="acc")
         for k in range(EARLY):
             for m in range(4):
-                project_close(k, m)
+                token_part(k, m, True)
+        for k in range(EARLY):
+            for m in range(4):
+                position_part(k, m, False)
                 project_out(k, m)
 
         s_ps, neg, e, t_ps, e_t = {}, {}, {}, {}, {}
@@ -298,9 +302,10 @@ def tile_mytransformer_b_kernel(tc, table, w_tok, pos, w_pos, bq, bv, mask, w_o,
             if t < len(belt) and len(belt[t]) == 2:
                 k, m = belt[t]
                 for i in range(UNIT):
-                    project_open(k, m + i, wide, "wide")
+                    p_ps[k, m + i] = wide.tile([P, PIECE], F32, name="p_ps", tag="wide")
+                    position_part(k, m + i, True)
                 for i in range(UNIT):
-                    project_close(k, m + i)
+                    token_part(k, m + i, False)
                 for i in range(UNIT):
                     project_out(k, m + i)
             x = due(t, LAG_FLIP)

@@ -31,7 +31,7 @@ LAG_OUT = LAG_COPY + AHEAD
 LAG_STORE = LAG_OUT + 1
 EARLY = 2
 UNIT = 2
-FIRST_UNIT = 9
+FIRST_UNIT = 10
 UNIT_EVERY = 3
 
 PAIRS = TOKENS * (TOKENS + 1) // 2
@@ -42,7 +42,7 @@ BYTES = (2 * (P * WORDS + 2 * P * 4 * P + P * TOKENS + 4 * P * P) + 4 * (5 * P) 
 
 def tile_mytransformer_b_kernel(tc, table, w_tok, pos, w_pos, bq, bv, mask, w_o, b_o, offs, out):
     nc = tc.nc
-    block_order = [1, 3, 5, 7, 6, 4, 2, 0, 9, 11, 13, 15, 14, 12, 10, 8]
+    block_order = [5, 7, 6, 4, 3, 2, 1, 0, 9, 11, 13, 15, 14, 12, 10, 8]
     with (
         tc.tile_pool(name="held", bufs=1) as held,
         tc.tile_pool(name="span", bufs=4) as span,
@@ -262,6 +262,10 @@ def tile_mytransformer_b_kernel(tc, table, w_tok, pos, w_pos, bq, bv, mask, w_o,
             return None
 
         for t in range(len(belt) + LAG_STORE + 1):
+            x = due(t, LAG_FLIP)
+            if x:
+                flips(*x)
+                flips_out(*x, t % 2 == 1)
             x = due(t, LAG_EXP)
             if x:
                 exponentials(*x)
@@ -280,9 +284,6 @@ def tile_mytransformer_b_kernel(tc, table, w_tok, pos, w_pos, bq, bv, mask, w_o,
             x = due(t, LAG_STORE, ends_block)
             if x:
                 store(x[0])
-            x = due(t, LAG_FLIP)
-            if x:
-                flips(*x)
             x = due(t, LAG_SUM)
             if x:
                 weighted_sum(*x)
@@ -308,6 +309,3 @@ def tile_mytransformer_b_kernel(tc, table, w_tok, pos, w_pos, bq, bv, mask, w_o,
                     token_part(k, m + i, False)
                 for i in range(UNIT):
                     project_out(k, m + i)
-            x = due(t, LAG_FLIP)
-            if x:
-                flips_out(*x, t % 2 == 1)

@@ -10,6 +10,8 @@ WORDS = 1024
 TOKENS = 2048
 HEADS = 2
 BLOCKS = TOKENS // P
+HALF = P // HEADS
+HALVES = P // HALF
 PIECE = 512
 PIECES = TOKENS // PIECE
 KEY, VAL = HEADS, HEADS + 1
@@ -87,12 +89,16 @@ def tile_mytransformer_b_kernel(tc, table, w_tok, pos, w_pos, bq, bv, mask, w_o,
         nc.vector.memset(bias[:], 0.0)
         nc.vector.tensor_copy(bias[:, 0:HEADS], bq_sb[:])
         nc.vector.tensor_copy(bias[:, VAL:VAL + 1], bv_sb[:])
-        penalty = held.tile([P, BLOCKS, P], BF16, name="penalty")
+        penalty = held.tile([P, BLOCKS, HALVES, HEADS, HALF], BF16, name="penalty")
         for b in block_order:
-            nc.gpsimd.tensor_scalar(out=penalty[:, b, :], in0=mask_sb[:, b, :], scalar1=-1.0, scalar2=MASKED,
-                                    op0=ALU.add, op1=ALU.mult)
+            for a in range(HEADS):
+                nc.gpsimd.tensor_scalar(out=penalty[:, b, :, a, :],
+                                        in0=mask_sb[:, b, :].rearrange("p (i q) -> p i q", i=HALVES),
+                                        scalar1=-1.0, scalar2=MASKED, op0=ALU.add, op1=ALU.mult)
 
-        proj = held.tile([P, 4, TOKENS], BF16, name="proj")
+        queries = held.tile([P, BLOCKS, HALVES, HEADS, HALF], BF16, name="queries")
+        keys = held.tile([P, TOKENS], BF16, name="keys")
+        values = held.tile([P, TOKENS], BF16, name="values")
         val_t = held.tile([P, BLOCKS, VPITCH], BF16, name="val_t")
         nc.vector.memset(val_t[:], 1.0)
         p_ps = {}
@@ -106,18 +112,21 @@ def tile_mytransformer_b_kernel(tc, table, w_tok, pos, w_pos, bq, bv, mask, w_o,
             nc.tensor.matmul(p_ps[k, m][:], w_tok_sb[:, m * P:(m + 1) * P], picked, start=first, stop=not first)
 
         def project_out(k, m):
-            cols = slice(k * PIECE, (k + 1) * PIECE)
-            if m % 2 == 0:
-                nc.scalar.activation(out=proj[:, m, cols], in_=p_ps[k, m][:], func=FUNC.Identity,
-                                     bias=bias[:, m:m + 1])
+            if m < HEADS:
+                to = queries[:, k * PER:(k + 1) * PER, :, m, :]
+                source = p_ps[k, m][:].rearrange("p (b i q) -> p b i q", b=PER, i=HALVES)
             else:
-                nc.vector.tensor_scalar(out=proj[:, m, cols], in0=p_ps[k, m][:], scalar1=bias[:, m:m + 1],
-                                        scalar2=None, op0=ALU.add)
+                to = (keys if m == KEY else values)[:, k * PIECE:(k + 1) * PIECE]
+                source = p_ps[k, m][:]
+            if m < HEADS:
+                nc.scalar.activation(out=to, in_=source, func=FUNC.Identity, bias=bias[:, m:m + 1])
+            else:
+                nc.vector.tensor_scalar(out=to, in0=source, scalar1=bias[:, m:m + 1], scalar2=None, op0=ALU.add)
 
         def flip_values(k):
             v_ps = flip.tile([P, PIECE], BF16, name="v_ps", tag="flip")
             for i in range(PER):
-                nc.tensor.transpose(v_ps[:, i * P:(i + 1) * P], proj[:, VAL, (k * PER + i) * P:(k * PER + i + 1) * P],
+                nc.tensor.transpose(v_ps[:, i * P:(i + 1) * P], values[:, (k * PER + i) * P:(k * PER + i + 1) * P],
                                     ident[:])
             nc.scalar.copy(val_t[:, k * PER:(k + 1) * PER, 0:P], v_ps[:].rearrange("p (b d) -> p b d", b=PER))
 
@@ -144,92 +153,100 @@ def tile_mytransformer_b_kernel(tc, table, w_tok, pos, w_pos, bq, bv, mask, w_o,
         def blocks_of(qb, s):
             return min(SPAN, qb + 1 - s * SPAN)
 
-        def halves_of(qb, s):
-            n = blocks_of(qb, s)
-            return [(h, s * SPAN + h * PER, min(PER, n - h * PER) * P) for h in range((n + PER - 1) // PER)]
+        def keys_of(qb, i):
+            return qb * P + (i + 1) * HALF
 
-        def ends_row(qb, a, s):
+        def width_of(qb, i, s):
+            return min(SPAN * P, keys_of(qb, i) - s * SPAN * P)
+
+        def banks_of(qb, i, s):
+            width = width_of(qb, i, s)
+            return [(h, s * SPAN * P + h * PIECE, min(PIECE, width - h * PIECE)) for h in range((width + PIECE - 1) // PIECE)]
+
+        def ends_row(qb, i, s):
             return s == spans_of(qb) - 1
 
-        def ends_block(qb, a, s):
-            return a == HEADS - 1 and s == spans_of(qb) - 1
+        def ends_block(qb, i, s):
+            return i == HALVES - 1 and s == spans_of(qb) - 1
 
-        def score_matmuls(qb, a, s):
-            for h, b0, width in halves_of(qb, s):
-                on_diagonal = b0 * P + width == (qb + 1) * P
-                s_ps[qb, a, s, h] = wide.tile([P, PIECE], F32, name="s_ps", tag="wide")
-                nc.tensor.matmul(s_ps[qb, a, s, h][:, :width], proj[:, a, qb * P:(qb + 1) * P],
-                                 proj[:, KEY, b0 * P:b0 * P + width], start=True, stop=not on_diagonal)
+        def score_matmuls(qb, i, s):
+            for h, k0, width in banks_of(qb, i, s):
+                on_diagonal = k0 + width == keys_of(qb, i)
+                s_ps[qb, i, s, h] = wide.tile([P, PIECE], F32, name="s_ps", tag="wide")
+                nc.tensor.matmul(s_ps[qb, i, s, h][:, :width], queries[:, qb, i, :, :],
+                                 keys[:, k0:k0 + width], start=True, stop=not on_diagonal)
                 if on_diagonal:
-                    nc.tensor.matmul(s_ps[qb, a, s, h][:, width - P:width], penalty[:, qb, :], ident[:],
-                                     start=False, stop=True)
+                    nc.tensor.matmul(s_ps[qb, i, s, h][:, width - HALF:width], penalty[:, qb, i, :, :],
+                                     ident[:, i * HALF:(i + 1) * HALF], start=False, stop=True)
 
-        def scores_out(qb, a, s):
+        def scores_out(qb, i, s):
             if s == 0:
-                low[qb, a] = small.tile([P, PIECES], F32, name="low")
-            neg[qb, a, s] = span.tile([P, SPAN * P], F32, name="neg", bufs=LAG_EXP + 2)
-            for h, b0, width in halves_of(qb, s):
-                nc.vector.tensor_scalar(out=neg[qb, a, s][:, h * PIECE:h * PIECE + width],
-                                        in0=s_ps[qb, a, s, h][:, :width], scalar1=-SCALE, scalar2=None,
-                                        op0=ALU.mult, op1=ALU.min, accum_out=low[qb, a][:, b0 // PER:b0 // PER + 1])
+                low[qb, i] = small.tile([P, PIECES], F32, name="low")
+            neg[qb, i, s] = span.tile([P, SPAN * P], F32, name="neg", bufs=LAG_EXP + 2)
+            for h, k0, width in banks_of(qb, i, s):
+                nc.vector.tensor_scalar(out=neg[qb, i, s][:, h * PIECE:h * PIECE + width],
+                                        in0=s_ps[qb, i, s, h][:, :width], scalar1=-SCALE, scalar2=None,
+                                        op0=ALU.mult, op1=ALU.min, accum_out=low[qb, i][:, k0 // PIECE:k0 // PIECE + 1])
 
-        def row_minimum(qb, a):
-            lowest[qb, a] = small.tile([P, 1], F32, name="lowest")
-            nc.vector.tensor_reduce(out=lowest[qb, a][:], in_=low[qb, a][:, :(qb + PER) // PER],
+        def row_minimum(qb, i):
+            lowest[qb, i] = small.tile([P, 1], F32, name="lowest")
+            nc.vector.tensor_reduce(out=lowest[qb, i][:], in_=low[qb, i][:, :(qb + PER) // PER],
                                     axis=mybir.AxisListType.X, op=ALU.min)
 
-        def exponentials(qb, a, s):
-            width = blocks_of(qb, s) * P
-            e[qb, a, s] = span.tile([P, SPAN * P], BF16, name="e", bufs=AHEAD + 2)
-            nc.scalar.activation(out=e[qb, a, s][:, :width], in_=neg[qb, a, s][:, :width], func=FUNC.Exp,
-                                 bias=lowest[qb, a][:, 0:1], scale=-1.0)
+        def exponentials(qb, i, s):
+            width = width_of(qb, i, s)
+            e[qb, i, s] = e_ring[belt.index((qb, i, s)) % len(e_ring)]
+            if width < blocks_of(qb, s) * P:
+                nc.gpsimd.memset(e[qb, i, s][:, width:width + HALF], 0.0)
+            nc.scalar.activation(out=e[qb, i, s][:, :width], in_=neg[qb, i, s][:, :width], func=FUNC.Exp,
+                                 bias=lowest[qb, i][:, 0:1], scale=-1.0)
 
-        def flips(qb, a, s):
-            t_ps[qb, a, s] = flip.tile([P, SPAN * P], BF16, name="t_ps", tag="flip")
-            for i in range(blocks_of(qb, s)):
-                nc.tensor.transpose(t_ps[qb, a, s][:, i * P:(i + 1) * P], e[qb, a, s][:, i * P:(i + 1) * P], ident[:])
+        def flips(qb, i, s):
+            t_ps[qb, i, s] = flip.tile([P, SPAN * P], BF16, name="t_ps", tag="flip")
+            for n in range(blocks_of(qb, s)):
+                nc.tensor.transpose(t_ps[qb, i, s][:, n * P:(n + 1) * P], e[qb, i, s][:, n * P:(n + 1) * P], ident[:])
 
-        def flips_out(qb, a, s, by_scalar):
+        def flips_out(qb, i, s, by_scalar):
             width = blocks_of(qb, s) * P
-            e_t[qb, a, s] = span.tile([P, SPAN * P], BF16, name="e_t", bufs=AHEAD + 2)
+            e_t[qb, i, s] = span.tile([P, SPAN * P], BF16, name="e_t", bufs=AHEAD + 2)
             if by_scalar:
-                nc.scalar.copy(e_t[qb, a, s][:, :width], t_ps[qb, a, s][:, :width])
+                nc.scalar.copy(e_t[qb, i, s][:, :width], t_ps[qb, i, s][:, :width])
             else:
-                nc.vector.tensor_copy(e_t[qb, a, s][:, :width], t_ps[qb, a, s][:, :width])
+                nc.vector.tensor_copy(e_t[qb, i, s][:, :width], t_ps[qb, i, s][:, :width])
 
-        def weighted_sum(qb, a, s):
-            if a == 0 and s == 0:
-                acc[qb] = sums.tile([P, HEADS, VPITCH], F32, name="acc")
-            for i in range(blocks_of(qb, s)):
-                b = s * SPAN + i
-                nc.tensor.matmul(acc[qb][:, a, 0:P + 1], e_t[qb, a, s][:, i * P:(i + 1) * P], val_t[:, b, 0:P + 1],
+        def weighted_sum(qb, i, s):
+            if i == 0 and s == 0:
+                acc[qb] = sums.tile([P, HALVES, VPITCH], F32, name="acc")
+            for n in range(blocks_of(qb, s)):
+                b = s * SPAN + n
+                nc.tensor.matmul(acc[qb][:, i, 0:P + 1], e_t[qb, i, s][:, n * P:(n + 1) * P], val_t[:, b, 0:P + 1],
                                  start=b == 0, stop=b == qb)
 
         def reciprocals(qb):
-            inv[qb] = small.tile([P, HEADS, 1], F32, name="inv")
+            inv[qb] = small.tile([P, HALVES, 1], F32, name="inv")
             nc.vector.reciprocal(inv[qb][:], acc[qb][:, :, P:P + 1])
 
         def divide(qb):
-            att_q[qb] = small.tile([P, HEADS, P], BF16, name="att_q")
-            for a in range(HEADS):
-                nc.scalar.activation(out=att_q[qb][:, a, :], in_=acc[qb][:, a, 0:P], func=FUNC.Copy,
-                                     scale=inv[qb][:, a, :])
+            att_q[qb] = small.tile([P, HALVES, P], BF16, name="att_q")
+            for i in range(HALVES):
+                nc.scalar.activation(out=att_q[qb][:, i, :], in_=acc[qb][:, i, 0:P], func=FUNC.Copy,
+                                     scale=inv[qb][:, i, :])
 
         def att_flips(qb):
             a_ps[qb] = wide.tile([P, PIECE], BF16, name="a_ps", tag="wide")
-            for a in range(HEADS):
-                nc.tensor.transpose(a_ps[qb][:, a * P:(a + 1) * P], att_q[qb][:, a, :], ident[:])
+            for i in range(HALVES):
+                nc.tensor.transpose(a_ps[qb][:, i * P:(i + 1) * P], att_q[qb][:, i, :], ident[:])
 
         def att_out(qb):
-            att[qb] = small.tile([P, HEADS * P], BF16, name="att")
-            nc.vector.tensor_copy(att[qb][:], a_ps[qb][:, :HEADS * P])
+            att[qb] = small.tile([P, HALVES, HEADS, HALF], BF16, name="att")
+            nc.vector.tensor_copy(att[qb][:], a_ps[qb][:, :HALVES * P].rearrange("p (i a q) -> p i a q", i=HALVES, a=HEADS))
 
         def output_matmuls(qb):
             o_ps[qb] = wide.tile([P, PIECE], F32, name="o_ps", tag="wide")
             for h in range(2):
                 for a in range(HEADS):
                     nc.tensor.matmul(o_ps[qb][:, h * P:(h + 1) * P], w_o_sb[:, a, h * P:(h + 1) * P],
-                                     att[qb][:, a * P:(a + 1) * P], start=a == 0, stop=a == HEADS - 1)
+                                     att[qb][:, :, a, :], start=a == 0, stop=a == HEADS - 1)
 
         out_view = out.rearrange("(h p) j -> p h j", p=P)
 
@@ -242,11 +259,12 @@ def tile_mytransformer_b_kernel(tc, table, w_tok, pos, w_pos, bq, bv, mask, w_o,
 
         units = [(k, m) for k in range(EARLY, PIECES) for m in range(0, 4, UNIT)]
         belt = []
-        for r, (qb, a) in enumerate([(qb, a) for qb in block_order for a in range(HEADS)]):
-            i, rest = divmod(r - FIRST_UNIT, UNIT_EVERY)
-            if rest == 0 and 0 <= i < len(units):
-                belt.append(units[i])
-            belt.extend([(qb, a, s) for s in range(spans_of(qb))])
+        for r, (qb, i) in enumerate([(qb, i) for qb in block_order for i in range(HALVES)]):
+            u, rest = divmod(r - FIRST_UNIT, UNIT_EVERY)
+            if rest == 0 and 0 <= u < len(units):
+                belt.append(units[u])
+            belt.extend([(qb, i, s) for s in range(spans_of(qb))])
+        e_ring = [held.tile([P, SPAN * P], BF16, name=f"e_{n}") for n in range(AHEAD + 2)]
 
         def due(t, lag, only=None):
             if not 0 <= t - lag < len(belt) or len(belt[t - lag]) != 3:

@@ -20,6 +20,7 @@ VPITCH = 136
 SCALE = P ** -0.5
 MASKED = 1.0e9
 SPAN = 8
+PENALTIES_AHEAD = 3
 LAG_MIN = 1
 LAG_EXP = 3
 AHEAD = 3
@@ -31,10 +32,9 @@ LAG_ATT = LAG_DIV + AHEAD
 LAG_COPY = LAG_ATT + 1
 LAG_OUT = LAG_COPY + AHEAD
 LAG_STORE = LAG_OUT + 1
-EARLY = 2
-UNIT = 2
-FIRST_UNIT = 10
-UNIT_EVERY = 3
+BLOCK_ORDER = [3, 2, 7, 6, 5, 4, 1, 11, 10, 9, 8, 12, 13, 14, 15, 0]
+PROJECTED_BEHIND = {3: (1, [KEY, 0]), 2: (1, [1, VAL]), 4: (2, [0, 1]), 1: (2, [KEY, VAL]),
+                    11: (3, [0]), 10: (3, [1]), 9: (3, [KEY]), 8: (3, [VAL])}
 
 PAIRS = TOKENS * (TOKENS + 1) // 2
 FLOPS = 2 * (2 * P) * (4 * P) * TOKENS + HEADS * 2 * (2 * P * PAIRS) + 2 * (2 * P) * (2 * P) * TOKENS
@@ -44,7 +44,6 @@ BYTES = (2 * (P * WORDS + 2 * P * 4 * P + P * TOKENS + 4 * P * P) + 4 * (5 * P) 
 
 def tile_mytransformer_b_kernel(tc, table, w_tok, pos, w_pos, bq, bv, mask, w_o, b_o, offs, out):
     nc = tc.nc
-    block_order = [5, 7, 6, 4, 3, 2, 1, 0, 9, 11, 13, 15, 14, 12, 10, 8]
     with (
         tc.tile_pool(name="held", bufs=1) as held,
         tc.tile_pool(name="span", bufs=4) as span,
@@ -68,19 +67,18 @@ def tile_mytransformer_b_kernel(tc, table, w_tok, pos, w_pos, bq, bv, mask, w_o,
             nc.sync.dma_start(pos_sb[:, k * PIECE:(k + 1) * PIECE], pos[:, k * PIECE:(k + 1) * PIECE])
 
         nc.sync.dma_start(offsets[:], offs)
-        nc.scalar.dma_start(w_tok_sb[:], w_tok)
-        nc.sync.dma_start(table_sb[:, :WORDS // 2], table[:, :WORDS // 2])
-        nc.scalar.dma_start(table_sb[:, WORDS // 2:], table[:, WORDS // 2:])
         nc.scalar.dma_start(w_pos_sb[:], w_pos)
-        for k in range(EARLY):
+        load_pos(0)
+        nc.scalar.dma_start(table_sb[:, WORDS // 2:], table[:, WORDS // 2:])
+        nc.sync.dma_start(table_sb[:, :WORDS // 2], table[:, :WORDS // 2])
+        nc.sync.dma_start(w_tok_sb[:], w_tok)
+        nc.sync.dma_start(bq_sb[:], bq.rearrange("(a p) o -> p (a o)", p=P))
+        nc.sync.dma_start(bv_sb[:], bv)
+        for k in range(1, PIECES):
             load_pos(k)
-        nc.scalar.dma_start(bq_sb[:], bq.rearrange("(a p) o -> p (a o)", p=P))
-        nc.scalar.dma_start(bv_sb[:], bv)
-        for k in range(EARLY, PIECES):
-            load_pos(k)
-        nc.scalar.dma_start(bo_sb[:], b_o.rearrange("(h p) o -> p (h o)", p=P))
+        nc.sync.dma_start(bo_sb[:], b_o.rearrange("(h p) o -> p (h o)", p=P))
         nc.gpsimd.dma_start(w_o_sb[:], w_o.rearrange("(a p) m -> p a m", p=P))
-        for b in block_order:
+        for b in BLOCK_ORDER:
             nc.sync.dma_start(mask_sb[:, b, :], mask[b * P:(b + 1) * P, b * P:(b + 1) * P])
 
         ident = held.tile([P, P], BF16, name="ident")
@@ -90,11 +88,14 @@ def tile_mytransformer_b_kernel(tc, table, w_tok, pos, w_pos, bq, bv, mask, w_o,
         nc.vector.tensor_copy(bias[:, 0:HEADS], bq_sb[:])
         nc.vector.tensor_copy(bias[:, VAL:VAL + 1], bv_sb[:])
         penalty = held.tile([P, BLOCKS, HALVES, HEADS, HALF], BF16, name="penalty")
-        for b in block_order:
-            for a in range(HEADS):
-                nc.gpsimd.tensor_scalar(out=penalty[:, b, :, a, :],
-                                        in0=mask_sb[:, b, :].rearrange("p (i q) -> p i q", i=HALVES),
-                                        scalar1=-1.0, scalar2=MASKED, op0=ALU.add, op1=ALU.mult)
+
+        def make_penalty(b):
+            lies = mask_sb[:, b, :].rearrange("p (i q) -> p i q", i=HALVES).unsqueeze(2)
+            nc.gpsimd.tensor_scalar(out=penalty[:, b, :, :, :], in0=lies.to_broadcast([P, HALVES, HEADS, HALF]),
+                                    scalar1=-1.0, scalar2=MASKED, op0=ALU.add, op1=ALU.mult)
+
+        for b in BLOCK_ORDER[:PENALTIES_AHEAD]:
+            make_penalty(b)
 
         queries = held.tile([P, BLOCKS, HALVES, HEADS, HALF], BF16, name="queries")
         keys = held.tile([P, TOKENS], BF16, name="keys")
@@ -130,18 +131,20 @@ def tile_mytransformer_b_kernel(tc, table, w_tok, pos, w_pos, bq, bv, mask, w_o,
                                     ident[:])
             nc.scalar.copy(val_t[:, k * PER:(k + 1) * PER, 0:P], v_ps[:].rearrange("p (b d) -> p b d", b=PER))
 
+        rows = [KEY, 0, 1, VAL]
         for m in range(4):
             p_ps[0, m] = wide.tile([P, PIECE], F32, name="p_ps", tag="wide")
         for m in range(2):
             p_ps[1, m] = flip.tile([P, PIECE], F32, name="p_ps", tag="flip")
             p_ps[1, m + 2] = sums.tile([P, PIECE], F32, name="p_ps", tag="acc")
-        for k in range(EARLY):
-            for m in range(4):
-                token_part(k, m, True)
-        for k in range(EARLY):
-            for m in range(4):
-                position_part(k, m, False)
-                project_out(k, m)
+        for m in rows:
+            position_part(0, m, True)
+        for m in rows:
+            token_part(0, m, False)
+        for m in rows:
+            token_part(1, m, True)
+        for m in rows:
+            project_out(0, m)
 
         s_ps, neg, e, t_ps, e_t = {}, {}, {}, {}, {}
         low, lowest = {}, {}
@@ -189,9 +192,18 @@ def tile_mytransformer_b_kernel(tc, table, w_tok, pos, w_pos, bq, bv, mask, w_o,
                                         op0=ALU.mult, op1=ALU.min, accum_out=low[qb, i][:, k0 // PIECE:k0 // PIECE + 1])
 
         def row_minimum(qb, i):
-            lowest[qb, i] = small.tile([P, 1], F32, name="lowest")
-            nc.vector.tensor_reduce(out=lowest[qb, i][:], in_=low[qb, i][:, :(qb + PER) // PER],
-                                    axis=mybir.AxisListType.X, op=ALU.min)
+            n = (qb + PER) // PER
+            least = low[qb, i]
+            if n == 1:
+                lowest[qb, i] = least[:, 0:1]
+                return
+            pair = small.tile([P, 2], F32, name="pair")
+            nc.gpsimd.tensor_scalar(out=pair[:, 0:1], in0=least[:, 0:1], scalar1=least[:, 1:2], scalar2=least[:, n - 1:n],
+                                    op0=ALU.min, op1=ALU.min)
+            lowest[qb, i] = pair[:, 0:1]
+            if n == 4:
+                nc.gpsimd.tensor_scalar(out=pair[:, 1:2], in0=pair[:, 0:1], scalar1=least[:, 2:3], scalar2=None, op0=ALU.min)
+                lowest[qb, i] = pair[:, 1:2]
 
         def exponentials(qb, i, s):
             width = width_of(qb, i, s)
@@ -199,7 +211,7 @@ def tile_mytransformer_b_kernel(tc, table, w_tok, pos, w_pos, bq, bv, mask, w_o,
             if width < blocks_of(qb, s) * P:
                 nc.gpsimd.memset(e[qb, i, s][:, width:width + HALF], 0.0)
             nc.scalar.activation(out=e[qb, i, s][:, :width], in_=neg[qb, i, s][:, :width], func=FUNC.Exp,
-                                 bias=lowest[qb, i][:, 0:1], scale=-1.0)
+                                 bias=lowest[qb, i], scale=-1.0)
 
         def flips(qb, i, s):
             t_ps[qb, i, s] = flip.tile([P, SPAN * P], BF16, name="t_ps", tag="flip")
@@ -253,17 +265,15 @@ def tile_mytransformer_b_kernel(tc, table, w_tok, pos, w_pos, bq, bv, mask, w_o,
         def store(qb):
             o_sb = small.tile([P, 2, P], F32, name="o_sb")
             for h in range(2):
-                nc.scalar.activation(out=o_sb[:, h, :], in_=o_ps[qb][:, h * P:(h + 1) * P], func=FUNC.Identity,
-                                     bias=bo_sb[:, h:h + 1])
+                nc.vector.tensor_scalar(out=o_sb[:, h, :], in0=o_ps[qb][:, h * P:(h + 1) * P], scalar1=bo_sb[:, h:h + 1],
+                                        scalar2=None, op0=ALU.add)
             nc.sync.dma_start(out_view[:, :, qb * P:(qb + 1) * P], o_sb[:])
 
-        units = [(k, m) for k in range(EARLY, PIECES) for m in range(0, 4, UNIT)]
         belt = []
-        for r, (qb, i) in enumerate([(qb, i) for qb in block_order for i in range(HALVES)]):
-            u, rest = divmod(r - FIRST_UNIT, UNIT_EVERY)
-            if rest == 0 and 0 <= u < len(units):
-                belt.append(units[u])
-            belt.extend([(qb, i, s) for s in range(spans_of(qb))])
+        for qb in BLOCK_ORDER:
+            belt.extend([(qb, i, s) for i in range(HALVES) for s in range(spans_of(qb))])
+            if qb in PROJECTED_BEHIND:
+                belt.append(PROJECTED_BEHIND[qb])
         e_ring = [held.tile([P, SPAN * P], BF16, name=f"e_{n}") for n in range(AHEAD + 2)]
 
         def due(t, lag, only=None):
@@ -273,9 +283,9 @@ def tile_mytransformer_b_kernel(tc, table, w_tok, pos, w_pos, bq, bv, mask, w_o,
             return x if only is None or only(*x) else None
 
         def values_due(t):
-            if 1 <= t <= EARLY:
-                return t - 1
-            if 0 <= t - AHEAD < len(belt) and len(belt[t - AHEAD]) == 2 and belt[t - AHEAD][1] + UNIT == 4:
+            if t == 1:
+                return 0
+            if 0 <= t - AHEAD < len(belt) and len(belt[t - AHEAD]) == 2 and VAL in belt[t - AHEAD][1]:
                 return belt[t - AHEAD][0]
             return None
 
@@ -316,14 +326,21 @@ def tile_mytransformer_b_kernel(tc, table, w_tok, pos, w_pos, bq, bv, mask, w_o,
                 output_matmuls(x[0])
             x = due(t, 0)
             if x:
+                n = BLOCK_ORDER.index(x[0]) + PENALTIES_AHEAD
+                if x[1] == 0 and x[2] == 0 and n < BLOCKS:
+                    make_penalty(BLOCK_ORDER[n])
                 score_matmuls(*x)
                 scores_out(*x)
             if t < len(belt) and len(belt[t]) == 2:
-                k, m = belt[t]
-                for i in range(UNIT):
-                    p_ps[k, m + i] = wide.tile([P, PIECE], F32, name="p_ps", tag="wide")
-                    position_part(k, m + i, True)
-                for i in range(UNIT):
-                    token_part(k, m + i, False)
-                for i in range(UNIT):
-                    project_out(k, m + i)
+                k, blocks = belt[t]
+                for m in blocks:
+                    if k == 1:
+                        position_part(1, m, False)
+                    else:
+                        p_ps[k, m] = wide.tile([P, PIECE], F32, name="p_ps", tag="wide")
+                        position_part(k, m, True)
+                if k != 1:
+                    for m in blocks:
+                        token_part(k, m, False)
+                for m in blocks:
+                    project_out(k, m)

@@ -193,17 +193,12 @@ def tile_mytransformer_b_kernel(tc, table, w_tok, pos, w_pos, bq, bv, mask, w_o,
 
         def row_minimum(qb, i):
             n = (qb + PER) // PER
-            least = low[qb, i]
             if n == 1:
-                lowest[qb, i] = least[:, 0:1]
+                lowest[qb, i] = low[qb, i][:, 0:1]
                 return
-            pair = small.tile([P, 2], F32, name="pair")
-            nc.gpsimd.tensor_scalar(out=pair[:, 0:1], in0=least[:, 0:1], scalar1=least[:, 1:2], scalar2=least[:, n - 1:n],
-                                    op0=ALU.min, op1=ALU.min)
-            lowest[qb, i] = pair[:, 0:1]
-            if n == 4:
-                nc.gpsimd.tensor_scalar(out=pair[:, 1:2], in0=pair[:, 0:1], scalar1=least[:, 2:3], scalar2=None, op0=ALU.min)
-                lowest[qb, i] = pair[:, 1:2]
+            least = small.tile([P, 1], F32, name="least")
+            nc.vector.tensor_reduce(out=least[:], in_=low[qb, i][:, :n], axis=mybir.AxisListType.X, op=ALU.min)
+            lowest[qb, i] = least[:]
 
         def exponentials(qb, i, s):
             width = width_of(qb, i, s)
@@ -265,8 +260,8 @@ def tile_mytransformer_b_kernel(tc, table, w_tok, pos, w_pos, bq, bv, mask, w_o,
         def store(qb):
             o_sb = small.tile([P, 2, P], F32, name="o_sb")
             for h in range(2):
-                nc.vector.tensor_scalar(out=o_sb[:, h, :], in0=o_ps[qb][:, h * P:(h + 1) * P], scalar1=bo_sb[:, h:h + 1],
-                                        scalar2=None, op0=ALU.add)
+                nc.scalar.activation(out=o_sb[:, h, :], in_=o_ps[qb][:, h * P:(h + 1) * P], func=FUNC.Identity,
+                                     bias=bo_sb[:, h:h + 1])
             nc.sync.dma_start(out_view[:, :, qb * P:(qb + 1) * P], o_sb[:])
 
         belt = []

@@ -32,9 +32,9 @@ LAG_ATT = LAG_DIV + AHEAD
 LAG_COPY = LAG_ATT + 1
 LAG_OUT = LAG_COPY + AHEAD
 LAG_STORE = LAG_OUT + 1
-BLOCK_ORDER = [3, 2, 7, 6, 5, 4, 1, 11, 10, 9, 8, 12, 13, 14, 15, 0]
-PROJECTED_BEHIND = {3: (1, [KEY, 0]), 2: (1, [1, VAL]), 4: (2, [0, 1]), 1: (2, [KEY, VAL]),
-                    11: (3, [0]), 10: (3, [1]), 9: (3, [KEY]), 8: (3, [VAL])}
+BLOCK_ORDER = [3, 2, 7, 6, 5, 4, 1, 11, 10, 9, 8, 15, 14, 13, 12, 0]
+PROJECTED_BEHIND = {3: (1, [KEY, 0]), 2: (1, [1, VAL]), 5: (2, [0, 1]), 1: (2, [KEY, VAL]),
+                    11: (3, [0]), 10: (3, [KEY]), 9: (3, [1]), 8: (3, [VAL])}
 
 PAIRS = TOKENS * (TOKENS + 1) // 2
 FLOPS = 2 * (2 * P) * (4 * P) * TOKENS + HEADS * 2 * (2 * P * PAIRS) + 2 * (2 * P) * (2 * P) * TOKENS
@@ -67,18 +67,20 @@ def tile_mytransformer_b_kernel(tc, table, w_tok, pos, w_pos, bq, bv, mask, w_o,
             nc.sync.dma_start(pos_sb[:, k * PIECE:(k + 1) * PIECE], pos[:, k * PIECE:(k + 1) * PIECE])
 
         nc.sync.dma_start(offsets[:], offs)
-        nc.scalar.dma_start(w_pos_sb[:], w_pos)
-        load_pos(0)
-        nc.scalar.dma_start(table_sb[:, WORDS // 2:], table[:, WORDS // 2:])
+        nc.scalar.dma_start(w_tok_sb[:], w_tok)
         nc.sync.dma_start(table_sb[:, :WORDS // 2], table[:, :WORDS // 2])
-        nc.sync.dma_start(w_tok_sb[:], w_tok)
-        nc.sync.dma_start(bq_sb[:], bq.rearrange("(a p) o -> p (a o)", p=P))
-        nc.sync.dma_start(bv_sb[:], bv)
-        for k in range(1, PIECES):
+        nc.scalar.dma_start(table_sb[:, WORDS // 2:], table[:, WORDS // 2:])
+        nc.scalar.dma_start(w_pos_sb[:], w_pos)
+        for k in range(2):
             load_pos(k)
-        nc.sync.dma_start(bo_sb[:], b_o.rearrange("(h p) o -> p (h o)", p=P))
+        nc.scalar.dma_start(bq_sb[:], bq.rearrange("(a p) o -> p (a o)", p=P))
+        nc.scalar.dma_start(bv_sb[:], bv)
         nc.gpsimd.dma_start(w_o_sb[:], w_o.rearrange("(a p) m -> p a m", p=P))
-        for b in BLOCK_ORDER:
+        nc.gpsimd.dma_start(bo_sb[:], b_o.rearrange("(h p) o -> p (h o)", p=P))
+        for n, b in enumerate(BLOCK_ORDER):
+            if n == PENALTIES_AHEAD + 1:
+                for k in range(2, PIECES):
+                    load_pos(k)
             nc.sync.dma_start(mask_sb[:, b, :], mask[b * P:(b + 1) * P, b * P:(b + 1) * P])
 
         ident = held.tile([P, P], BF16, name="ident")
@@ -137,13 +139,11 @@ def tile_mytransformer_b_kernel(tc, table, w_tok, pos, w_pos, bq, bv, mask, w_o,
         for m in range(2):
             p_ps[1, m] = flip.tile([P, PIECE], F32, name="p_ps", tag="flip")
             p_ps[1, m + 2] = sums.tile([P, PIECE], F32, name="p_ps", tag="acc")
+        for k in range(2):
+            for m in rows:
+                token_part(k, m, True)
         for m in rows:
-            position_part(0, m, True)
-        for m in rows:
-            token_part(0, m, False)
-        for m in rows:
-            token_part(1, m, True)
-        for m in rows:
+            position_part(0, m, False)
             project_out(0, m)
 
         s_ps, neg, e, t_ps, e_t = {}, {}, {}, {}, {}

@@ -32,9 +32,8 @@ LAG_ATT = LAG_DIV + AHEAD
 LAG_COPY = LAG_ATT + 1
 LAG_OUT = LAG_COPY + AHEAD
 LAG_STORE = LAG_OUT + 1
-BLOCK_ORDER = [3, 2, 7, 6, 5, 4, 1, 11, 10, 9, 8, 15, 14, 13, 12, 0]
-PROJECTED_BEHIND = {3: (1, [KEY, 0]), 2: (1, [1, VAL]), 5: (2, [0, 1]), 1: (2, [KEY, VAL]),
-                    11: (3, [0]), 10: (3, [KEY]), 9: (3, [1]), 8: (3, [VAL])}
+BLOCK_ORDER = [5, 7, 9, 11, 10, 8, 13, 15, 14, 12, 6, 4, 3, 2, 1, 0]
+PROJECTED_BEHIND = {9: 0, 11: KEY, 10: 1, 8: VAL}
 
 PAIRS = TOKENS * (TOKENS + 1) // 2
 FLOPS = 2 * (2 * P) * (4 * P) * TOKENS + HEADS * 2 * (2 * P * PAIRS) + 2 * (2 * P) * (2 * P) * TOKENS
@@ -67,11 +66,12 @@ def tile_mytransformer_b_kernel(tc, table, w_tok, pos, w_pos, bq, bv, mask, w_o,
             nc.sync.dma_start(pos_sb[:, k * PIECE:(k + 1) * PIECE], pos[:, k * PIECE:(k + 1) * PIECE])
 
         nc.sync.dma_start(offsets[:], offs)
+        load_pos(0)
+        nc.scalar.dma_start(w_pos_sb[:], w_pos)
         nc.scalar.dma_start(w_tok_sb[:], w_tok)
         nc.sync.dma_start(table_sb[:, :WORDS // 2], table[:, :WORDS // 2])
         nc.scalar.dma_start(table_sb[:, WORDS // 2:], table[:, WORDS // 2:])
-        nc.scalar.dma_start(w_pos_sb[:], w_pos)
-        for k in range(2):
+        for k in range(1, 3):
             load_pos(k)
         nc.scalar.dma_start(bq_sb[:], bq.rearrange("(a p) o -> p (a o)", p=P))
         nc.scalar.dma_start(bv_sb[:], bv)
@@ -79,8 +79,7 @@ def tile_mytransformer_b_kernel(tc, table, w_tok, pos, w_pos, bq, bv, mask, w_o,
         nc.gpsimd.dma_start(bo_sb[:], b_o.rearrange("(h p) o -> p (h o)", p=P))
         for n, b in enumerate(BLOCK_ORDER):
             if n == PENALTIES_AHEAD + 1:
-                for k in range(2, PIECES):
-                    load_pos(k)
+                load_pos(3)
             nc.sync.dma_start(mask_sb[:, b, :], mask[b * P:(b + 1) * P, b * P:(b + 1) * P])
 
         ident = held.tile([P, P], BF16, name="ident")
@@ -121,7 +120,7 @@ def tile_mytransformer_b_kernel(tc, table, w_tok, pos, w_pos, bq, bv, mask, w_o,
             else:
                 to = (keys if m == KEY else values)[:, k * PIECE:(k + 1) * PIECE]
                 source = p_ps[k, m][:]
-            if m < HEADS:
+            if m < HEADS and k > 0:
                 nc.scalar.activation(out=to, in_=source, func=FUNC.Identity, bias=bias[:, m:m + 1])
             else:
                 nc.vector.tensor_scalar(out=to, in0=source, scalar1=bias[:, m:m + 1], scalar2=None, op0=ALU.add)
@@ -139,12 +138,21 @@ def tile_mytransformer_b_kernel(tc, table, w_tok, pos, w_pos, bq, bv, mask, w_o,
         for m in range(2):
             p_ps[1, m] = flip.tile([P, PIECE], F32, name="p_ps", tag="flip")
             p_ps[1, m + 2] = sums.tile([P, PIECE], F32, name="p_ps", tag="acc")
-        for k in range(2):
-            for m in rows:
-                token_part(k, m, True)
         for m in rows:
-            position_part(0, m, False)
+            position_part(0, m, True)
+        for m in rows:
+            token_part(0, m, False)
+        for m in rows:
+            token_part(1, m, True)
+        for m in rows:
             project_out(0, m)
+        for m in rows:
+            p_ps[2, m] = wide.tile([P, PIECE], F32, name="p_ps", tag="wide")
+            token_part(2, m, True)
+        for k in (1, 2):
+            for m in rows:
+                position_part(k, m, False)
+                project_out(k, m)
 
         s_ps, neg, e, t_ps, e_t = {}, {}, {}, {}, {}
         low, lowest = {}, {}
@@ -268,7 +276,7 @@ def tile_mytransformer_b_kernel(tc, table, w_tok, pos, w_pos, bq, bv, mask, w_o,
         for qb in BLOCK_ORDER:
             belt.extend([(qb, i, s) for i in range(HALVES) for s in range(spans_of(qb))])
             if qb in PROJECTED_BEHIND:
-                belt.append(PROJECTED_BEHIND[qb])
+                belt.append((PIECES - 1, PROJECTED_BEHIND[qb]))
         e_ring = [held.tile([P, SPAN * P], BF16, name=f"e_{n}") for n in range(AHEAD + 2)]
 
         def due(t, lag, only=None):
@@ -278,9 +286,9 @@ def tile_mytransformer_b_kernel(tc, table, w_tok, pos, w_pos, bq, bv, mask, w_o,
             return x if only is None or only(*x) else None
 
         def values_due(t):
-            if t == 1:
-                return 0
-            if 0 <= t - AHEAD < len(belt) and len(belt[t - AHEAD]) == 2 and VAL in belt[t - AHEAD][1]:
+            if 1 <= t <= 3:
+                return t - 1
+            if 0 <= t - AHEAD < len(belt) and len(belt[t - AHEAD]) == 2 and belt[t - AHEAD][1] == VAL:
                 return belt[t - AHEAD][0]
             return None
 
@@ -327,15 +335,8 @@ def tile_mytransformer_b_kernel(tc, table, w_tok, pos, w_pos, bq, bv, mask, w_o,
                 score_matmuls(*x)
                 scores_out(*x)
             if t < len(belt) and len(belt[t]) == 2:
-                k, blocks = belt[t]
-                for m in blocks:
-                    if k == 1:
-                        position_part(1, m, False)
-                    else:
-                        p_ps[k, m] = wide.tile([P, PIECE], F32, name="p_ps", tag="wide")
-                        position_part(k, m, True)
-                if k != 1:
-                    for m in blocks:
-                        token_part(k, m, False)
-                for m in blocks:
-                    project_out(k, m)
+                k, m = belt[t]
+                p_ps[k, m] = wide.tile([P, PIECE], F32, name="p_ps", tag="wide")
+                position_part(k, m, True)
+                token_part(k, m, False)
+                project_out(k, m)

@@ -32,8 +32,8 @@ LAG_ATT = LAG_DIV + AHEAD
 LAG_COPY = LAG_ATT + 1
 LAG_OUT = LAG_COPY + AHEAD
 LAG_STORE = LAG_OUT + 1
-BLOCK_ORDER = [5, 7, 9, 11, 10, 8, 13, 15, 14, 12, 6, 4, 3, 2, 1, 0]
-PROJECTED_BEHIND = {9: 0, 11: KEY, 10: 1, 8: VAL}
+BLOCK_ORDER = [7, 11, 5, 6, 9, 10, 15, 14, 13, 12, 8, 4, 3, 2, 1, 0]
+PROJECTED_BEHIND = {5: 0, 6: KEY, 9: 1, 10: VAL}
 
 PAIRS = TOKENS * (TOKENS + 1) // 2
 FLOPS = 2 * (2 * P) * (4 * P) * TOKENS + HEADS * 2 * (2 * P * PAIRS) + 2 * (2 * P) * (2 * P) * TOKENS
@@ -193,7 +193,7 @@ def tile_mytransformer_b_kernel(tc, table, w_tok, pos, w_pos, bq, bv, mask, w_o,
         def scores_out(qb, i, s):
             if s == 0:
                 low[qb, i] = small.tile([P, PIECES], F32, name="low")
-            neg[qb, i, s] = span.tile([P, SPAN * P], F32, name="neg", bufs=LAG_EXP + 2)
+            neg[qb, i, s] = span.tile([P, SPAN * P], F32, name="neg", bufs=LAG_EXP + 1)
             for h, k0, width in banks_of(qb, i, s):
                 nc.vector.tensor_scalar(out=neg[qb, i, s][:, h * PIECE:h * PIECE + width],
                                         in0=s_ps[qb, i, s, h][:, :width], scalar1=-SCALE, scalar2=None,

@@ -161,18 +161,21 @@ def tile_mytransformer_b_kernel(tc, table, w_tok, pos, w_pos, bq, bv, mask, w_o,
         def spans_of(qb):
             return (qb + SPAN) // SPAN
 
+        def first_block(qb, s):
+            return s * (PER if qb + 1 < SPAN + PER else SPAN)
+
         def blocks_of(qb, s):
-            return min(SPAN, qb + 1 - s * SPAN)
+            return (first_block(qb, 1) if s + 1 < spans_of(qb) else qb + 1) - first_block(qb, s)
 
         def keys_of(qb, i):
             return qb * P + (i + 1) * HALF
 
         def width_of(qb, i, s):
-            return min(SPAN * P, keys_of(qb, i) - s * SPAN * P)
+            return min(blocks_of(qb, s) * P, keys_of(qb, i) - first_block(qb, s) * P)
 
         def banks_of(qb, i, s):
             width = width_of(qb, i, s)
-            return [(h, s * SPAN * P + h * PIECE, min(PIECE, width - h * PIECE)) for h in range((width + PIECE - 1) // PIECE)]
+            return [(h, first_block(qb, s) * P + h * PIECE, min(PIECE, width - h * PIECE)) for h in range((width + PIECE - 1) // PIECE)]
 
         def ends_row(qb, i, s):
             return s == spans_of(qb) - 1
@@ -233,7 +236,7 @@ def tile_mytransformer_b_kernel(tc, table, w_tok, pos, w_pos, bq, bv, mask, w_o,
             if i == 0 and s == 0:
                 acc[qb] = sums.tile([P, HALVES, VPITCH], F32, name="acc")
             for n in range(blocks_of(qb, s)):
-                b = s * SPAN + n
+                b = first_block(qb, s) + n
                 nc.tensor.matmul(acc[qb][:, i, 0:P + 1], e_t[qb, i, s][:, n * P:(n + 1) * P], val_t[:, b, 0:P + 1],
                                  start=b == 0, stop=b == qb)
 
@@ -296,7 +299,7 @@ def tile_mytransformer_b_kernel(tc, table, w_tok, pos, w_pos, bq, bv, mask, w_o,
             x = due(t, LAG_FLIP)
             if x:
                 flips(*x)
-                flips_out(*x, t % 2 == 1)
+                flips_out(*x, by_scalar=t % 2 == 1 and x[0] > PER)
             x = due(t, LAG_EXP)
             if x:
                 exponentials(*x)

@@ -120,7 +120,7 @@ def tile_mytransformer_b_kernel(tc, table, w_tok, pos, w_pos, bq, bv, mask, w_o,
             else:
                 to = (keys if m == KEY else values)[:, k * PIECE:(k + 1) * PIECE]
                 source = p_ps[k, m][:]
-            if m < HEADS and k > 0:
+            if m in (0, VAL) and k > 0:
                 nc.scalar.activation(out=to, in_=source, func=FUNC.Identity, bias=bias[:, m:m + 1])
             else:
                 nc.vector.tensor_scalar(out=to, in0=source, scalar1=bias[:, m:m + 1], scalar2=None, op0=ALU.add)

@@ -216,8 +216,10 @@ def tile_mytransformer_b_kernel(tc, table, w_tok, pos, w_pos, bq, bv, mask, w_o,
             e[qb, i, s] = e_ring[belt.index((qb, i, s)) % len(e_ring)]
             if width < blocks_of(qb, s) * P:
                 nc.gpsimd.memset(e[qb, i, s][:, width:width + HALF], 0.0)
-            nc.scalar.activation(out=e[qb, i, s][:, :width], in_=neg[qb, i, s][:, :width], func=FUNC.Exp,
-                                 bias=lowest[qb, i], scale=-1.0)
+            for k0 in range(0, width, PIECE):
+                k1 = min(k0 + PIECE, width)
+                nc.scalar.activation(out=e[qb, i, s][:, k0:k1], in_=neg[qb, i, s][:, k0:k1], func=FUNC.Exp,
+                                     bias=lowest[qb, i], scale=-1.0)
 
         def flips(qb, i, s):
             t_ps[qb, i, s] = flip.tile([P, SPAN * P], BF16, name="t_ps", tag="flip")

import concourse.mybir as mybir
from concourse.masks import make_identity

BF16, F32, U16 = mybir.dt.bfloat16, mybir.dt.float32, mybir.dt.uint16
ALU = mybir.AluOpType
FUNC = mybir.ActivationFunctionType

P = 128
WORDS = 1024
TOKENS = 2048
HEADS = 2
BLOCKS = TOKENS // P
HALF = P // HEADS
HALVES = P // HALF
PIECE = 512
PIECES = TOKENS // PIECE
KEY, VAL = HEADS, HEADS + 1
PER = PIECE // P
VPITCH = 136
SCALE = P ** -0.5
MASKED = 1.0e9
SPAN = 8
PENALTIES_AHEAD = 3
LAG_MIN = 1
LAG_EXP = 3
AHEAD = 3
LAG_FLIP = LAG_EXP + AHEAD
LAG_SUM = LAG_FLIP + AHEAD
LAG_INV = LAG_SUM + 1
LAG_DIV = LAG_INV + 1
LAG_ATT = LAG_DIV + AHEAD
LAG_COPY = LAG_ATT + 1
LAG_OUT = LAG_COPY + AHEAD
LAG_STORE = LAG_OUT + 1
BLOCK_ORDER = [7, 11, 5, 6, 9, 10, 15, 14, 13, 12, 8, 4, 3, 2, 1, 0]
PROJECTED_BEHIND = {5: 0, 6: KEY, 9: 1, 10: VAL}

PAIRS = TOKENS * (TOKENS + 1) // 2
FLOPS = 2 * (2 * P) * (4 * P) * TOKENS + HEADS * 2 * (2 * P * PAIRS) + 2 * (2 * P) * (2 * P) * TOKENS
BYTES = (2 * (P * WORDS + 2 * P * 4 * P + P * TOKENS + 4 * P * P) + 4 * (5 * P) + 2 * P * (TOKENS // 16)
         + 4 * BLOCKS * P * P + 4 * 2 * P * TOKENS)


def tile_mytransformer_b_kernel(tc, table, w_tok, pos, w_pos, bq, bv, mask, w_o, b_o, offs, out):
    nc = tc.nc
    with (
        tc.tile_pool(name="held", bufs=1) as held,
        tc.tile_pool(name="span", bufs=4) as span,
        tc.tile_pool(name="small", bufs=8) as small,
        tc.psum_pool(name="wide", bufs=4) as wide,
        tc.psum_pool(name="flip", bufs=2) as flip,
        tc.psum_pool(name="sums", bufs=2) as sums,
    ):
        table_sb = held.tile([P, WORDS], BF16, name="table_sb")
        offsets = held.tile([P, TOKENS // 16], U16, name="offsets")
        w_tok_sb = held.tile([P, 4 * P], BF16, name="w_tok_sb")
        w_pos_sb = held.tile([P, 4 * P], BF16, name="w_pos_sb")
        pos_sb = held.tile([P, TOKENS], BF16, name="pos_sb")
        w_o_sb = held.tile([P, HEADS, 2 * P], BF16, name="w_o_sb")
        bq_sb = held.tile([P, HEADS], F32, name="bq_sb")
        bv_sb = held.tile([P, 1], F32, name="bv_sb")
        bo_sb = held.tile([P, 2], F32, name="bo_sb")
        mask_sb = held.tile([P, BLOCKS, P], F32, name="mask_sb")

        def load_pos(k):
            nc.sync.dma_start(pos_sb[:, k * PIECE:(k + 1) * PIECE], pos[:, k * PIECE:(k + 1) * PIECE])

        nc.sync.dma_start(offsets[:], offs)
        load_pos(0)
        nc.scalar.dma_start(w_pos_sb[:], w_pos)
        nc.scalar.dma_start(w_tok_sb[:], w_tok)
        nc.sync.dma_start(table_sb[:, :WORDS // 2], table[:, :WORDS // 2])
        nc.scalar.dma_start(table_sb[:, WORDS // 2:], table[:, WORDS // 2:])
        for k in range(1, 3):
            load_pos(k)
        nc.scalar.dma_start(bq_sb[:], bq.rearrange("(a p) o -> p (a o)", p=P))
        nc.scalar.dma_start(bv_sb[:], bv)
        nc.gpsimd.dma_start(w_o_sb[:], w_o.rearrange("(a p) m -> p a m", p=P))
        nc.gpsimd.dma_start(bo_sb[:], b_o.rearrange("(h p) o -> p (h o)", p=P))
        for n, b in enumerate(BLOCK_ORDER):
            if n == PENALTIES_AHEAD + 1:
                load_pos(3)
            nc.sync.dma_start(mask_sb[:, b, :], mask[b * P:(b + 1) * P, b * P:(b + 1) * P])

        ident = held.tile([P, P], BF16, name="ident")
        make_identity(nc, ident[:])
        bias = held.tile([P, 4], F32, name="bias")
        nc.vector.memset(bias[:], 0.0)
        nc.vector.tensor_copy(bias[:, 0:HEADS], bq_sb[:])
        nc.vector.tensor_copy(bias[:, VAL:VAL + 1], bv_sb[:])
        penalty = held.tile([P, BLOCKS, HALVES, HEADS, HALF], BF16, name="penalty")

        def make_penalty(b):
            lies = mask_sb[:, b, :].rearrange("p (i q) -> p i q", i=HALVES).unsqueeze(2)
            nc.gpsimd.tensor_scalar(out=penalty[:, b, :, :, :], in0=lies.to_broadcast([P, HALVES, HEADS, HALF]),
                                    scalar1=-1.0, scalar2=MASKED, op0=ALU.add, op1=ALU.mult)

        for b in BLOCK_ORDER[:PENALTIES_AHEAD]:
            make_penalty(b)

        queries = held.tile([P, BLOCKS, HALVES, HEADS, HALF], BF16, name="queries")
        keys = held.tile([P, TOKENS], BF16, name="keys")
        values = held.tile([P, TOKENS], BF16, name="values")
        val_t = held.tile([P, BLOCKS, VPITCH], BF16, name="val_t")
        nc.vector.memset(val_t[:], 1.0)
        p_ps = {}

        def position_part(k, m, first):
            nc.tensor.matmul(p_ps[k, m][:], w_pos_sb[:, m * P:(m + 1) * P], pos_sb[:, k * PIECE:(k + 1) * PIECE],
                             start=first, stop=not first)

        def token_part(k, m, first):
            picked = table_sb[:].indirect(offsets[:, k * (PIECE // 16):(k + 1) * (PIECE // 16)])
            nc.tensor.matmul(p_ps[k, m][:], w_tok_sb[:, m * P:(m + 1) * P], picked, start=first, stop=not first)

        def project_out(k, m):
            if m < HEADS:
                to = queries[:, k * PER:(k + 1) * PER, :, m, :]
                source = p_ps[k, m][:].rearrange("p (b i q) -> p b i q", b=PER, i=HALVES)
            else:
                to = (keys if m == KEY else values)[:, k * PIECE:(k + 1) * PIECE]
                source = p_ps[k, m][:]
            if m in (0, VAL) and k > 0:
                nc.scalar.activation(out=to, in_=source, func=FUNC.Identity, bias=bias[:, m:m + 1])
            else:
                nc.vector.tensor_scalar(out=to, in0=source, scalar1=bias[:, m:m + 1], scalar2=None, op0=ALU.add)

        def flip_values(k):
            v_ps = flip.tile([P, PIECE], BF16, name="v_ps", tag="flip")
            for i in range(PER):
                nc.tensor.transpose(v_ps[:, i * P:(i + 1) * P], values[:, (k * PER + i) * P:(k * PER + i + 1) * P],
                                    ident[:])
            nc.scalar.copy(val_t[:, k * PER:(k + 1) * PER, 0:P], v_ps[:].rearrange("p (b d) -> p b d", b=PER))

        rows = [KEY, 0, 1, VAL]
        for m in range(4):
            p_ps[0, m] = wide.tile([P, PIECE], F32, name="p_ps", tag="wide")
        for m in range(2):
            p_ps[1, m] = flip.tile([P, PIECE], F32, name="p_ps", tag="flip")
            p_ps[1, m + 2] = sums.tile([P, PIECE], F32, name="p_ps", tag="acc")
        for m in rows:
            position_part(0, m, True)
        for m in rows:
            token_part(0, m, False)
        for m in rows:
            token_part(1, m, True)
        for m in rows:
            project_out(0, m)
        for m in rows:
            p_ps[2, m] = wide.tile([P, PIECE], F32, name="p_ps", tag="wide")
            token_part(2, m, True)
        for k in (1, 2):
            for m in rows:
                position_part(k, m, False)
                project_out(k, m)

        s_ps, neg, e, t_ps, e_t = {}, {}, {}, {}, {}
        low, lowest = {}, {}
        acc, inv, att_q, a_ps, att, o_ps = {}, {}, {}, {}, {}, {}

        def spans_of(qb):
            return (qb + SPAN) // SPAN

        def first_block(qb, s):
            return s * (PER if qb + 1 < SPAN + PER else SPAN)

        def blocks_of(qb, s):
            return (first_block(qb, 1) if s + 1 < spans_of(qb) else qb + 1) - first_block(qb, s)

        def keys_of(qb, i):
            return qb * P + (i + 1) * HALF

        def width_of(qb, i, s):
            return min(blocks_of(qb, s) * P, keys_of(qb, i) - first_block(qb, s) * P)

        def banks_of(qb, i, s):
            width = width_of(qb, i, s)
            return [(h, first_block(qb, s) * P + h * PIECE, min(PIECE, width - h * PIECE)) for h in range((width + PIECE - 1) // PIECE)]

        def ends_row(qb, i, s):
            return s == spans_of(qb) - 1

        def ends_block(qb, i, s):
            return i == HALVES - 1 and s == spans_of(qb) - 1

        def score_matmuls(qb, i, s):
            for h, k0, width in banks_of(qb, i, s):
                on_diagonal = k0 + width == keys_of(qb, i)
                s_ps[qb, i, s, h] = wide.tile([P, PIECE], F32, name="s_ps", tag="wide")
                nc.tensor.matmul(s_ps[qb, i, s, h][:, :width], queries[:, qb, i, :, :],
                                 keys[:, k0:k0 + width], start=True, stop=not on_diagonal)
                if on_diagonal:
                    nc.tensor.matmul(s_ps[qb, i, s, h][:, width - HALF:width], penalty[:, qb, i, :, :],
                                     ident[:, i * HALF:(i + 1) * HALF], start=False, stop=True)

        def scores_out(qb, i, s):
            if s == 0:
                low[qb, i] = small.tile([P, PIECES], F32, name="low")
            neg[qb, i, s] = span.tile([P, SPAN * P], F32, name="neg", bufs=LAG_EXP + 1)
            for h, k0, width in banks_of(qb, i, s):
                nc.vector.tensor_scalar(out=neg[qb, i, s][:, h * PIECE:h * PIECE + width],
                                        in0=s_ps[qb, i, s, h][:, :width], scalar1=-SCALE, scalar2=None,
                                        op0=ALU.mult, op1=ALU.min, accum_out=low[qb, i][:, k0 // PIECE:k0 // PIECE + 1])

        def row_minimum(qb, i):
            n = (qb + PER) // PER
            if n == 1:
                lowest[qb, i] = low[qb, i][:, 0:1]
                return
            least = small.tile([P, 1], F32, name="least")
            nc.vector.tensor_reduce(out=least[:], in_=low[qb, i][:, :n], axis=mybir.AxisListType.X, op=ALU.min)
            lowest[qb, i] = least[:]

        def exponentials(qb, i, s):
            width = width_of(qb, i, s)
            e[qb, i, s] = e_ring[belt.index((qb, i, s)) % len(e_ring)]
            if width < blocks_of(qb, s) * P:
                nc.gpsimd.memset(e[qb, i, s][:, width:width + HALF], 0.0)
            for k0 in range(0, width, PIECE):
                k1 = min(k0 + PIECE, width)
                nc.scalar.activation(out=e[qb, i, s][:, k0:k1], in_=neg[qb, i, s][:, k0:k1], func=FUNC.Exp,
                                     bias=lowest[qb, i], scale=-1.0)

        def flips(qb, i, s):
            t_ps[qb, i, s] = flip.tile([P, SPAN * P], BF16, name="t_ps", tag="flip")
            for n in range(blocks_of(qb, s)):
                nc.tensor.transpose(t_ps[qb, i, s][:, n * P:(n + 1) * P], e[qb, i, s][:, n * P:(n + 1) * P], ident[:])

        def flips_out(qb, i, s, by_scalar):
            width = blocks_of(qb, s) * P
            e_t[qb, i, s] = span.tile([P, SPAN * P], BF16, name="e_t", bufs=AHEAD + 2)
            if by_scalar:
                nc.scalar.copy(e_t[qb, i, s][:, :width], t_ps[qb, i, s][:, :width])
            else:
                nc.vector.tensor_copy(e_t[qb, i, s][:, :width], t_ps[qb, i, s][:, :width])

        def weighted_sum(qb, i, s):
            if i == 0 and s == 0:
                acc[qb] = sums.tile([P, HALVES, VPITCH], F32, name="acc")
            for n in range(blocks_of(qb, s)):
                b = first_block(qb, s) + n
                nc.tensor.matmul(acc[qb][:, i, 0:P + 1], e_t[qb, i, s][:, n * P:(n + 1) * P], val_t[:, b, 0:P + 1],
                                 start=b == 0, stop=b == qb)

        def reciprocals(qb):
            inv[qb] = small.tile([P, HALVES, 1], F32, name="inv")
            nc.vector.reciprocal(inv[qb][:], acc[qb][:, :, P:P + 1])

        def divide(qb):
            att_q[qb] = small.tile([P, HALVES, P], BF16, name="att_q")
            for i in range(HALVES):
                nc.scalar.activation(out=att_q[qb][:, i, :], in_=acc[qb][:, i, 0:P], func=FUNC.Copy,
                                     scale=inv[qb][:, i, :])

        def att_flips(qb):
            a_ps[qb] = wide.tile([P, PIECE], BF16, name="a_ps", tag="wide")
            for i in range(HALVES):
                nc.tensor.transpose(a_ps[qb][:, i * P:(i + 1) * P], att_q[qb][:, i, :], ident[:])

        def att_out(qb):
            att[qb] = small.tile([P, HALVES, HEADS, HALF], BF16, name="att")
            nc.vector.tensor_copy(att[qb][:], a_ps[qb][:, :HALVES * P].rearrange("p (i a q) -> p i a q", i=HALVES, a=HEADS))

        def output_matmuls(qb):
            o_ps[qb] = wide.tile([P, PIECE], F32, name="o_ps", tag="wide")
            for h in range(2):
                for a in range(HEADS):
                    nc.tensor.matmul(o_ps[qb][:, h * P:(h + 1) * P], w_o_sb[:, a, h * P:(h + 1) * P],
                                     att[qb][:, :, a, :], start=a == 0, stop=a == HEADS - 1)

        out_view = out.rearrange("(h p) j -> p h j", p=P)

        def store(qb):
            o_sb = small.tile([P, 2, P], F32, name="o_sb")
            for h in range(2):
                nc.scalar.activation(out=o_sb[:, h, :], in_=o_ps[qb][:, h * P:(h + 1) * P], func=FUNC.Identity,
                                     bias=bo_sb[:, h:h + 1])
            nc.sync.dma_start(out_view[:, :, qb * P:(qb + 1) * P], o_sb[:])

        belt = []
        for qb in BLOCK_ORDER:
            belt.extend([(qb, i, s) for i in range(HALVES) for s in range(spans_of(qb))])
            if qb in PROJECTED_BEHIND:
                belt.append((PIECES - 1, PROJECTED_BEHIND[qb]))
        e_ring = [held.tile([P, SPAN * P], BF16, name=f"e_{n}") for n in range(AHEAD + 2)]

        def due(t, lag, only=None):
            if not 0 <= t - lag < len(belt) or len(belt[t - lag]) != 3:
                return None
            x = belt[t - lag]
            return x if only is None or only(*x) else None

        def values_due(t):
            if 1 <= t <= 3:
                return t - 1
            if 0 <= t - AHEAD < len(belt) and len(belt[t - AHEAD]) == 2 and belt[t - AHEAD][1] == VAL:
                return belt[t - AHEAD][0]
            return None

        for t in range(len(belt) + LAG_STORE + 1):
            x = due(t, LAG_FLIP)
            if x:
                flips(*x)
                flips_out(*x, by_scalar=t % 2 == 1 and x[0] > PER)
            x = due(t, LAG_EXP)
            if x:
                exponentials(*x)
            x = due(t, LAG_MIN, ends_row)
            if x:
                row_minimum(x[0], x[1])
            x = due(t, LAG_INV, ends_block)
            if x:
                reciprocals(x[0])
            x = due(t, LAG_DIV, ends_block)
            if x:
                divide(x[0])
            x = due(t, LAG_COPY, ends_block)
            if x:
                att_out(x[0])
            x = due(t, LAG_STORE, ends_block)
            if x:
                store(x[0])
            x = due(t, LAG_SUM)
            if x:
                weighted_sum(*x)
            k = values_due(t)
            if k is not None:
                flip_values(k)
            x = due(t, LAG_ATT, ends_block)
            if x:
                att_flips(x[0])
            x = due(t, LAG_OUT, ends_block)
            if x:
                output_matmuls(x[0])
            x = due(t, 0)
            if x:
                n = BLOCK_ORDER.index(x[0]) + PENALTIES_AHEAD
                if x[1] == 0 and x[2] == 0 and n < BLOCKS:
                    make_penalty(BLOCK_ORDER[n])
                score_matmuls(*x)
                scores_out(*x)
            if t < len(belt) and len(belt[t]) == 2:
                k, m = belt[t]
                p_ps[k, m] = wide.tile([P, PIECE], F32, name="p_ps", tag="wide")
                position_part(k, m, True)
                token_part(k, m, False)
                project_out(k, m)
